import numpy as np
import ml_dtypes


def mxq(x, axis, fmt="e4m3"):
    dtype, down = {"e4m3": (ml_dtypes.float8_e4m3fn, 7), "e5m2": (ml_dtypes.float8_e5m2, 14)}[fmt]
    v = np.moveaxis(np.asarray(x, np.float32).astype(ml_dtypes.bfloat16).astype(np.float64), axis, -1)
    blocks = v.reshape(v.shape[:-1] + (-1, 32))
    amax = np.abs(blocks).max(-1, keepdims=True)
    byte = np.maximum(np.where(amax > 0, np.frexp(amax)[1] - 1 + 127, 0) - down, 1)
    scale = np.exp2(byte - 127.0)
    codes = (blocks / scale).astype(np.float32).astype(dtype).astype(np.float64)
    return np.moveaxis((codes * scale).reshape(v.shape), -1, axis)


WIDE = False


def mx_kscale(k):
    if not WIDE:
        return np.ones(k)
    levels = np.array([10, -10, 5, -5, 0])
    if k % 512:
        return np.exp2(np.random.permutation(np.resize(levels, k // 32))).repeat(32)
    a = np.empty((k // 512, 16))
    for p in range(k // 512):
        a[p, :8] = np.random.permutation(np.resize(levels, 8))
        for g in range(8):
            far = levels[np.abs(levels - a[p, g]) >= 10]
            a[p, g + 8] = far[np.random.randint(len(far))]
    return np.exp2(a.ravel()).repeat(32)


BF16 = ml_dtypes.bfloat16


def bf(x):
    return np.asarray(x, np.float32).astype(BF16)


def f64(x):
    return np.asarray(x).astype(np.float64)


B, T, E, H, DK, C = 4, 1024, 512, 4, 128, 512
DV = 2 * DK
F = H * DV
EPS = 1e-5


def setup_inputs():
    s, t = mx_kscale(E), mx_kscale(F)
    o = np.random.standard_normal((B, T, H, DV)) * 5.0 * np.exp(0.5 * np.random.standard_normal((B, T, H, 1)))
    return {"o_ret": bf(o),
            "x": bf(np.random.standard_normal((B, T, E)) * s),
            "Wg": bf(np.random.standard_normal((E, F)) / np.sqrt(E) / s[:, None] * t),
            "gn_weight": bf(1.0 + 0.1 * np.random.standard_normal(DV)),
            "Wo": bf(np.random.standard_normal((F, E)) / np.sqrt(F) / t[:, None])}


def reference(o_ret, x, Wg, gn_weight, Wo):
    o = f64(o_ret)
    rms = np.sqrt(np.mean(o * o, axis=-1, keepdims=True) + EPS)
    o = o / rms * f64(gn_weight)
    g = mxq(f64(x), 2, "e4m3") @ mxq(f64(Wg), 0, "e4m3")
    h = o.reshape(B, T, F) * g
    return mxq(h, 2, "e4m3") @ mxq(f64(Wo), 0, "e4m3")

@@ -1,0 +1,286 @@
+from contextlib import ExitStack
+
+import concourse.mybir as mybir
+from concourse.masks import make_identity
+
+F32 = mybir.dt.float32
+BF16 = mybir.dt.bfloat16
+U32 = mybir.dt.uint32
+U8 = mybir.dt.uint8
+FP8X4 = mybir.dt.float8_e4m3fn_x4
+
+P = 128
+PACK = 4
+K_PASS = P * PACK
+BANK = 512
+
+TOKENS = 4 * 1024
+E = 512
+HEADS = 4
+DV = 256
+F = HEADS * DV
+EPS = 1e-5
+
+TILES = TOKENS // P
+GROUP = 4
+GROUPS = TILES // GROUP
+F_BANKS = F // BANK
+F_PASSES = F // K_PASS
+HEADS_PER_BANK = BANK // DV
+HEAD_ROWS = DV // PACK
+
+FLOPS = 2 * TOKENS * E * F + 2 * TOKENS * F * E
+
+SQUARES_LEAD = 6
+INVERT_RMS_LEAD = 5
+X_TRANSPOSE_LEAD = 4
+X_COPY_LEAD = 3
+X_QUANTISE_LEAD = 2
+GATE_MATMUL_LEAD = 1
+GATE_MULTIPLY_LEAD = 0
+H_TRANSPOSE_LEAD = -1
+H_SCALE_LEAD = -1
+H_QUANTISE_LEAD = -2
+OUT_MATMUL_LEAD = -2
+OUT_COPY_LEAD = -3
+FIRST_STEP = -SQUARES_LEAD
+LAST_STEP = TILES - 1 - OUT_COPY_LEAD
+
+
+def tile_multiscaleretention_pc_t_kernel(tc, o_ret, x, Wg, gn_weight, Wo, out):
+    nc = tc.nc
+    mult = mybir.AluOpType.mult
+    func = mybir.ActivationFunctionType
+
+    x_dram = x.flatten_outer_dims().rearrange("(n p i) e -> n p (i e)", p=P, i=GROUP)
+    o_dram = o_ret.rearrange("b t h d -> (b t) (h d)").rearrange(
+        "(n p i) f -> n p (i f)", p=P, i=GROUP
+    )
+    out_dram = out.flatten_outer_dims().rearrange("(n p i) e -> n p (i e)", p=P, i=GROUP)
+
+    with ExitStack() as ctx:
+        keep = ctx.enter_context(tc.tile_pool(name="keep", bufs=1))
+        stream = ctx.enter_context(tc.tile_pool(name="stream", bufs=3))
+        psum = ctx.enter_context(tc.psum_pool(name="psum", bufs=2))
+
+        x_sb = [keep.tile([P, GROUP * E], BF16, name="x_sb%d" % grp) for grp in range(GROUPS)]
+        o_sb = [keep.tile([P, GROUP * F], BF16, name="o_sb%d" % grp) for grp in range(GROUPS)]
+        wg_raw = keep.tile([P, PACK, F], BF16)
+        wo_raw = keep.tile([P, F_PASSES, PACK, E], BF16)
+        gn_word = keep.tile([P, PACK], BF16)
+
+        nc.sync.dma_start(out=o_sb[0][:], in_=o_dram[0])
+        nc.sync.dma_start(out=wg_raw[:], in_=Wg.rearrange("(p j) f -> p j f", j=PACK))
+        nc.sync.dma_start(out=x_sb[0][:], in_=x_dram[0])
+        with nc.allow_non_contiguous_dma(reason="4 elements to a partition"):
+            for a in range(HEADS_PER_BANK):
+                nc.sync.dma_start(
+                    out=gn_word[a * HEAD_ROWS : (a + 1) * HEAD_ROWS, :],
+                    in_=gn_weight.rearrange("(p t) -> p t", t=PACK),
+                )
+        nc.sync.dma_start(out=wo_raw[:], in_=Wo.rearrange("(c p j) e -> p c j e", p=P, j=PACK))
+        for grp in range(1, GROUPS):
+            nc.sync.dma_start(out=x_sb[grp][:], in_=x_dram[grp])
+            nc.sync.dma_start(out=o_sb[grp][:], in_=o_dram[grp])
+
+        identity = keep.tile([P, P], F32)
+        make_identity(nc, identity[:])
+        eps = keep.tile([P, 1], F32)
+        nc.vector.memset(eps[:], EPS)
+
+        wg_grouped = keep.tile([P, F, PACK], BF16, align_bytes=64)
+        wg_codes = keep.tile([P, F], U32, align_bytes=64)
+        wg_scales = keep.tile([P, F], U8, align_bytes=64)
+        wo_grouped = keep.tile([P, F_PASSES, E, PACK], BF16, align_bytes=64)
+        wo_codes = keep.tile([P, F_PASSES, E], U32, align_bytes=64)
+        wo_scales = keep.tile([P, F_PASSES, E], U8, align_bytes=64)
+
+        def quantise_wg():
+            for n in range(F_BANKS):
+                cols = slice(n * BANK, (n + 1) * BANK)
+                nc.vector.tensor_copy(
+                    out=wg_grouped[:, cols, :].rearrange("p (t m) j -> p t m j", t=PACK),
+                    in_=wg_raw[:, :, cols].rearrange("p j (m t) -> p t m j", t=PACK),
+                )
+            for n in range(F_BANKS):
+                cols = slice(n * BANK, (n + 1) * BANK)
+                nc.vector.quantize_mx(
+                    out=wg_codes[:, cols].bitcast(FP8X4),
+                    scales=wg_scales[:, cols],
+                    in_=wg_grouped[:, cols, :].rearrange("p f t -> p (f t)"),
+                )
+
+        def quantise_wo():
+            for c in range(F_PASSES):
+                nc.vector.tensor_copy(
+                    out=wo_grouped[:, c, :, :],
+                    in_=wo_raw[:, c, :, :].rearrange("p j e -> p e j"),
+                )
+            for c in range(F_PASSES):
+                nc.vector.quantize_mx(
+                    out=wo_codes[:, c, :].bitcast(FP8X4),
+                    scales=wo_scales[:, c, :],
+                    in_=wo_grouped[:, c, :, :].rearrange("p e t -> p (e t)"),
+                )
+
+        sums, rms, inv_rms = {}, {}, {}
+        x_t, x_grouped, x_codes, x_scales = {}, {}, {}, {}
+        g_ps, h_f32, h_t, h_grouped, h_codes, h_scales = {}, {}, {}, {}, {}, {}
+        out_ps = {}
+
+        def sum_squares(j):
+            grp, i = divmod(j, GROUP)
+            if i == 0:
+                sums[grp] = stream.tile([P, GROUP * HEADS], F32, name="sums")
+            for head in range(HEADS):
+                squares = stream.tile([P, DV], BF16, name="squares")
+                nc.scalar.activation(
+                    out=squares[:],
+                    in_=o_sb[grp][:, i * F + head * DV : i * F + (head + 1) * DV],
+                    func=func.Square,
+                    accum_out=sums[grp][:, i * HEADS + head : i * HEADS + head + 1],
+                )
+            if i == GROUP - 1:
+                rms[grp] = stream.tile([P, GROUP * HEADS], F32, name="rms")
+                nc.scalar.activation(
+                    out=rms[grp][:], in_=sums[grp][:], func=func.Sqrt, scale=1.0 / DV, bias=eps[:]
+                )
+
+        def invert_rms(j):
+            grp, i = divmod(j, GROUP)
+            if i == GROUP - 1:
+                inv_rms[grp] = stream.tile([P, GROUP * HEADS], F32, name="inv_rms")
+                nc.vector.reciprocal(out=inv_rms[grp][:], in_=rms[grp][:])
+
+        def transpose_x(j):
+            grp, i = divmod(j, GROUP)
+            words = x_sb[grp][:].bitcast(F32)
+            x_t[j] = psum.tile([P, 2, P], F32, name="x_t")
+            for u in range(2):
+                first = i * (E // 2) + u
+                nc.tensor.transpose(
+                    x_t[j][:, u, :], words[:, first : (i + 1) * (E // 2) : 2], identity[:]
+                )
+
+        def copy_x(j):
+            x_grouped[j] = stream.tile([P, P * PACK], BF16, name="x_grouped", align_bytes=64)
+            nc.scalar.copy(
+                out=x_grouped[j][:].bitcast(F32).rearrange("p (r u) -> p r u", u=2),
+                in_=x_t[j][:].rearrange("p u r -> p r u"),
+            )
+
+        def quantise_x(j):
+            x_codes[j] = stream.tile([P, P], U32, name="x_codes", align_bytes=64)
+            x_scales[j] = stream.tile([P, P], U8, name="x_scales", align_bytes=64)
+            nc.vector.quantize_mx(
+                out=x_codes[j][:].bitcast(FP8X4), scales=x_scales[j][:], in_=x_grouped[j][:]
+            )
+
+        def gate_matmul(j):
+            g_ps[j] = []
+            for n in range(F_BANKS):
+                cols = slice(n * BANK, (n + 1) * BANK)
+                bank = psum.tile([P, BANK], F32, name="g_ps")
+                nc.tensor.matmul_mx(
+                    out=bank[:],
+                    lhsT=x_codes[j][:].bitcast(FP8X4),
+                    lhsT_scale=x_scales[j][:],
+                    rhs=wg_codes[:, cols].bitcast(FP8X4),
+                    rhs_scale=wg_scales[:, cols],
+                    start=True,
+                    stop=True,
+                )
+                g_ps[j].append(bank)
+
+        def gate_multiply(j):
+            grp, i = divmod(j, GROUP)
+            h_f32[j] = stream.tile([P, F], F32, name="h_f32")
+            for head in range(HEADS):
+                n, a = divmod(head, HEADS_PER_BANK)
+                rows = slice(a * HEAD_ROWS, (a + 1) * HEAD_ROWS)
+                o_head = o_sb[grp][:, i * F + head * DV : i * F + (head + 1) * DV]
+                h_bank = h_f32[j][:, n * BANK : (n + 1) * BANK]
+                nc.vector.scalar_tensor_tensor(
+                    out=h_bank.rearrange("p (t m) -> p t m", t=PACK)[:, :, rows],
+                    in0=g_ps[j][n][:].rearrange("p (t m) -> p t m", t=PACK)[:, :, rows],
+                    scalar=inv_rms[grp][:, i * HEADS + head : i * HEADS + head + 1],
+                    in1=o_head.rearrange("p (m t) -> p t m", t=PACK),
+                    op0=mult,
+                    op1=mult,
+                )
+
+        def transpose_h(j):
+            h_t[j] = []
+            for c in range(F_PASSES):
+                bank = psum.tile([P, PACK, P], F32, name="h_t")
+                for t in range(PACK):
+                    first = c * K_PASS + t * P
+                    nc.tensor.transpose(
+                        bank[:, t, :], h_f32[j][:, first : first + P], identity[:]
+                    )
+                h_t[j].append(bank)
+
+        def scale_h(j):
+            h_grouped[j] = stream.tile([P, F_PASSES, P, PACK], BF16, name="h_grouped", align_bytes=64)
+            for c in range(F_PASSES):
+                nc.vector.tensor_tensor(
+                    out=h_grouped[j][:, c, :, :],
+                    in0=h_t[j][c][:].rearrange("p t r -> p r t"),
+                    in1=gn_word[:].unsqueeze(1).to_broadcast([P, P, PACK]),
+                    op=mult,
+                )
+
+        def quantise_h(j):
+            h_codes[j] = stream.tile([P, F_PASSES * P], U32, name="h_codes", align_bytes=64)
+            h_scales[j] = stream.tile([P, F_PASSES * P], U8, name="h_scales", align_bytes=64)
+            nc.vector.quantize_mx(
+                out=h_codes[j][:].bitcast(FP8X4),
+                scales=h_scales[j][:],
+                in_=h_grouped[j][:].rearrange("p c r t -> p (c r t)"),
+            )
+
+        def out_matmul(j):
+            out_ps[j] = psum.tile([P, E], F32, name="out_ps")
+            for c in range(F_PASSES):
+                tokens = slice(c * P, (c + 1) * P)
+                nc.tensor.matmul_mx(
+                    out=out_ps[j][:],
+                    lhsT=h_codes[j][:, tokens].bitcast(FP8X4),
+                    lhsT_scale=h_scales[j][:, tokens],
+                    rhs=wo_codes[:, c, :].bitcast(FP8X4),
+                    rhs_scale=wo_scales[:, c, :],
+                    start=(c == 0),
+                    stop=(c == F_PASSES - 1),
+                )
+
+        def copy_out(j):
+            grp, i = divmod(j, GROUP)
+            out_sb = stream.tile([P, E], F32, name="out_sb")
+            nc.scalar.copy(out=out_sb[:], in_=out_ps[j][:])
+            nc.sync.dma_start(out=out_dram[grp][:, i * E : (i + 1) * E], in_=out_sb[:])
+
+        def run(stage, j):
+            if 0 <= j < TILES:
+                stage(j)
+
+        def pipeline_step(step):
+            run(transpose_x, step + X_TRANSPOSE_LEAD)
+            run(transpose_h, step + H_TRANSPOSE_LEAD)
+            run(copy_x, step + X_COPY_LEAD)
+            run(copy_out, step + OUT_COPY_LEAD)
+            run(sum_squares, step + SQUARES_LEAD)
+            run(gate_multiply, step + GATE_MULTIPLY_LEAD)
+            run(gate_matmul, step + GATE_MATMUL_LEAD)
+            run(invert_rms, step + INVERT_RMS_LEAD)
+            run(quantise_x, step + X_QUANTISE_LEAD)
+            run(quantise_h, step + H_QUANTISE_LEAD)
+            run(out_matmul, step + OUT_MATMUL_LEAD)
+            run(scale_h, step + H_SCALE_LEAD)
+
+        with tc.manual_schedule():
+            quantise_wg()
+            for step in range(FIRST_STEP, 1):
+                pipeline_step(step)
+            quantise_wo()
+            for step in range(1, LAST_STEP + 1):
+                pipeline_step(step)

@@ -24,27 +24,11 @@ EPS = 1e-5
 TILES = TOKENS // P
 GROUP = 4
 GROUPS = TILES // GROUP
-F_BANKS = F // BANK
-F_PASSES = F // K_PASS
-HEADS_PER_BANK = BANK // DV
+PAIR = 2
 HEAD_ROWS = DV // PACK
+HEADS_PER_PASS = K_PASS // DV
 
 FLOPS = 2 * TOKENS * E * F + 2 * TOKENS * F * E
-
-SQUARES_LEAD = 6
-INVERT_RMS_LEAD = 5
-X_TRANSPOSE_LEAD = 4
-X_COPY_LEAD = 3
-X_QUANTISE_LEAD = 2
-GATE_MATMUL_LEAD = 1
-GATE_MULTIPLY_LEAD = 0
-H_TRANSPOSE_LEAD = -1
-H_SCALE_LEAD = -1
-H_QUANTISE_LEAD = -2
-OUT_MATMUL_LEAD = -2
-OUT_COPY_LEAD = -3
-FIRST_STEP = -SQUARES_LEAD
-LAST_STEP = TILES - 1 - OUT_COPY_LEAD
 
 
 def tile_multiscaleretention_pc_t_kernel(tc, o_ret, x, Wg, gn_weight, Wo, out):
@@ -61,178 +45,247 @@ def tile_multiscaleretention_pc_t_kernel(tc, o_ret, x, Wg, gn_weight, Wo, out):
     with ExitStack() as ctx:
         keep = ctx.enter_context(tc.tile_pool(name="keep", bufs=1))
         stream = ctx.enter_context(tc.tile_pool(name="stream", bufs=3))
-        psum = ctx.enter_context(tc.psum_pool(name="psum", bufs=2))
+        psum = ctx.enter_context(tc.psum_pool(name="psum", bufs=1))
 
         x_sb = [keep.tile([P, GROUP * E], BF16, name="x_sb%d" % grp) for grp in range(GROUPS)]
         o_sb = [keep.tile([P, GROUP * F], BF16, name="o_sb%d" % grp) for grp in range(GROUPS)]
-        wg_raw = keep.tile([P, PACK, F], BF16)
-        wo_raw = keep.tile([P, F_PASSES, PACK, E], BF16)
+        wg_raw = [keep.tile([P, PACK, BANK], BF16, name="wg_raw%d" % n) for n in range(2)]
+        wo_raw = [keep.tile([P, PACK, E], BF16, name="wo_raw%d" % c) for c in range(2)]
         gn_word = keep.tile([P, PACK], BF16)
-
-        nc.sync.dma_start(out=o_sb[0][:], in_=o_dram[0])
-        nc.sync.dma_start(out=wg_raw[:], in_=Wg.rearrange("(p j) f -> p j f", j=PACK))
-        nc.sync.dma_start(out=x_sb[0][:], in_=x_dram[0])
-        with nc.allow_non_contiguous_dma(reason="4 elements to a partition"):
-            for a in range(HEADS_PER_BANK):
-                nc.sync.dma_start(
-                    out=gn_word[a * HEAD_ROWS : (a + 1) * HEAD_ROWS, :],
-                    in_=gn_weight.rearrange("(p t) -> p t", t=PACK),
-                )
-        nc.sync.dma_start(out=wo_raw[:], in_=Wo.rearrange("(c p j) e -> p c j e", p=P, j=PACK))
-        for grp in range(1, GROUPS):
-            nc.sync.dma_start(out=x_sb[grp][:], in_=x_dram[grp])
-            nc.sync.dma_start(out=o_sb[grp][:], in_=o_dram[grp])
-
+        gn_row = keep.tile([P, DV], BF16)
+        ones = keep.tile([P, P], BF16)
+        gn_pairs = keep.tile([P, BANK], BF16)
         identity = keep.tile([P, P], F32)
-        make_identity(nc, identity[:])
         eps = keep.tile([P, 1], F32)
-        nc.vector.memset(eps[:], EPS)
-
+        warm = keep.tile([P, 1], F32)
         wg_grouped = keep.tile([P, F, PACK], BF16, align_bytes=64)
         wg_codes = keep.tile([P, F], U32, align_bytes=64)
         wg_scales = keep.tile([P, F], U8, align_bytes=64)
-        wo_grouped = keep.tile([P, F_PASSES, E, PACK], BF16, align_bytes=64)
-        wo_codes = keep.tile([P, F_PASSES, E], U32, align_bytes=64)
-        wo_scales = keep.tile([P, F_PASSES, E], U8, align_bytes=64)
+        wo_grouped = keep.tile([P, 2, E, PACK], BF16, align_bytes=64)
+        wo_codes = keep.tile([P, 2, E], U32, align_bytes=64)
+        wo_scales = keep.tile([P, 2, E], U8, align_bytes=64)
 
-        def quantise_wg():
-            for n in range(F_BANKS):
-                cols = slice(n * BANK, (n + 1) * BANK)
+        def load_x(grp, first, last):
+            cols = slice(first * E, last * E)
+            nc.sync.dma_start(out=x_sb[grp][:, cols], in_=x_dram[grp][:, cols])
+
+        def load_o(grp, first, last):
+            cols = slice(first * F, last * F)
+            nc.sync.dma_start(out=o_sb[grp][:, cols], in_=o_dram[grp][:, cols])
+
+        def load_wg(n):
+            cols = slice(n * BANK, (n + 1) * BANK)
+            nc.sync.dma_start(
+                out=wg_raw[n][:], in_=Wg.rearrange("(p j) f -> p j f", j=PACK)[:, :, cols]
+            )
+
+        def load_small():
+            nc.sync.dma_start(out=gn_row[0:1, :], in_=gn_weight.unsqueeze(0))
+            with nc.allow_non_contiguous_dma(reason="4 elements to a partition"):
+                for a in range(HEADS_PER_PASS):
+                    nc.sync.dma_start(
+                        out=gn_word[a * HEAD_ROWS : (a + 1) * HEAD_ROWS, :],
+                        in_=gn_weight.rearrange("(p t) -> p t", t=PACK),
+                    )
+
+        def load_wo(c):
+            nc.sync.dma_start(
+                out=wo_raw[c][:], in_=Wo.rearrange("(c p j) e -> c p j e", p=P, j=PACK)[c]
+            )
+
+        def pairs(ap):
+            return ap.rearrange("p (u h) -> p u h", u=2)
+
+        def group_wg_pairs():
+            for u in range(2):
                 nc.vector.tensor_copy(
-                    out=wg_grouped[:, cols, :].rearrange("p (t m) j -> p t m j", t=PACK),
-                    in_=wg_raw[:, :, cols].rearrange("p j (m t) -> p t m j", t=PACK),
-                )
-            for n in range(F_BANKS):
-                cols = slice(n * BANK, (n + 1) * BANK)
-                nc.vector.quantize_mx(
-                    out=wg_codes[:, cols].bitcast(FP8X4),
-                    scales=wg_scales[:, cols],
-                    in_=wg_grouped[:, cols, :].rearrange("p f t -> p (f t)"),
+                    out=wg_grouped[:, u * DV : (u + 1) * DV, :].rearrange(
+                        "p (m e) j -> p m e j", e=2
+                    ),
+                    in_=wg_raw[0][:].rearrange("p j (m u e) -> p u m e j", u=2, e=2)[:, u],
                 )
 
-        def quantise_wo():
-            for c in range(F_PASSES):
-                nc.vector.tensor_copy(
-                    out=wo_grouped[:, c, :, :],
-                    in_=wo_raw[:, c, :, :].rearrange("p j e -> p e j"),
-                )
-            for c in range(F_PASSES):
-                nc.vector.quantize_mx(
-                    out=wo_codes[:, c, :].bitcast(FP8X4),
-                    scales=wo_scales[:, c, :],
-                    in_=wo_grouped[:, c, :, :].rearrange("p e t -> p (e t)"),
+        def group_wg_singles():
+            nc.vector.tensor_copy(
+                out=wg_grouped[:, BANK:F, :].rearrange("p (t m) j -> p t m j", t=PACK),
+                in_=wg_raw[1][:].rearrange("p j (m t) -> p t m j", t=PACK),
+            )
+
+        def quantise_wg(n):
+            cols = slice(n * BANK, (n + 1) * BANK)
+            nc.vector.quantize_mx(
+                out=wg_codes[:, cols].bitcast(FP8X4),
+                scales=wg_scales[:, cols],
+                in_=wg_grouped[:, cols, :].rearrange("p f t -> p (f t)"),
+            )
+
+        def group_wo(c):
+            nc.vector.tensor_copy(
+                out=wo_grouped[:, c, :, :], in_=wo_raw[c][:].rearrange("p j e -> p e j")
+            )
+
+        def quantise_wo(c):
+            nc.vector.quantize_mx(
+                out=wo_codes[:, c, :].bitcast(FP8X4),
+                scales=wo_scales[:, c, :],
+                in_=wo_grouped[:, c, :, :].rearrange("p e t -> p (e t)"),
+            )
+
+        def spread_gn():
+            spread = psum.tile([P, DV], F32, name="spread", tag="out_ps", bufs=2)
+            nc.tensor.matmul(spread[:], lhsT=ones[:], rhs=gn_row[:], start=True, stop=True)
+            for a in range(HEADS_PER_PASS):
+                nc.scalar.copy(
+                    out=gn_pairs[:].rearrange("p (u a m e) -> p a u m e", u=2, a=2, e=2)[:, a],
+                    in_=spread[:].rearrange("p (m u e) -> p u m e", u=2, e=2),
                 )
 
         sums, rms, inv_rms = {}, {}, {}
         x_t, x_grouped, x_codes, x_scales = {}, {}, {}, {}
-        g_ps, h_f32, h_t, h_grouped, h_codes, h_scales = {}, {}, {}, {}, {}, {}
-        out_ps = {}
+        g_ps, o_gn, h_pairs, h_singles, hp_t, hs_t = {}, {}, {}, {}, {}, {}
+        h_grouped, h_codes, h_scales, out_ps = {}, {}, {}, {}
 
-        def sum_squares(j):
+        def o_head(j, head):
             grp, i = divmod(j, GROUP)
-            if i == 0:
-                sums[grp] = stream.tile([P, GROUP * HEADS], F32, name="sums")
-            for head in range(HEADS):
+            first = i * F + head * DV
+            return o_sb[grp][:, first : first + DV]
+
+        def inv_rms_col(j, head):
+            pair, i = divmod(j, PAIR)
+            return inv_rms[pair][:, i * HEADS + head : i * HEADS + head + 1]
+
+        def sum_squares(j, heads):
+            pair, i = divmod(j, PAIR)
+            if i == 0 and heads[0] == 0:
+                sums[pair] = stream.tile([P, PAIR * HEADS], F32, name="sums")
+            for head in heads:
                 squares = stream.tile([P, DV], BF16, name="squares")
                 nc.scalar.activation(
                     out=squares[:],
-                    in_=o_sb[grp][:, i * F + head * DV : i * F + (head + 1) * DV],
+                    in_=o_head(j, head),
                     func=func.Square,
-                    accum_out=sums[grp][:, i * HEADS + head : i * HEADS + head + 1],
-                )
-            if i == GROUP - 1:
-                rms[grp] = stream.tile([P, GROUP * HEADS], F32, name="rms")
-                nc.scalar.activation(
-                    out=rms[grp][:], in_=sums[grp][:], func=func.Sqrt, scale=1.0 / DV, bias=eps[:]
+                    accum_out=sums[pair][:, i * HEADS + head : i * HEADS + head + 1],
                 )
 
-        def invert_rms(j):
-            grp, i = divmod(j, GROUP)
-            if i == GROUP - 1:
-                inv_rms[grp] = stream.tile([P, GROUP * HEADS], F32, name="inv_rms")
-                nc.vector.reciprocal(out=inv_rms[grp][:], in_=rms[grp][:])
+        def root(pair):
+            rms[pair] = stream.tile([P, PAIR * HEADS], F32, name="rms")
+            nc.scalar.activation(
+                out=rms[pair][:], in_=sums[pair][:], func=func.Sqrt, scale=1.0 / DV, bias=eps[:]
+            )
 
-        def transpose_x(j):
-            grp, i = divmod(j, GROUP)
-            words = x_sb[grp][:].bitcast(F32)
-            x_t[j] = psum.tile([P, 2, P], F32, name="x_t")
-            for u in range(2):
-                first = i * (E // 2) + u
-                nc.tensor.transpose(
-                    x_t[j][:, u, :], words[:, first : (i + 1) * (E // 2) : 2], identity[:]
-                )
+        def invert(pair):
+            inv_rms[pair] = stream.tile([P, PAIR * HEADS], F32, name="inv_rms")
+            nc.vector.reciprocal(out=inv_rms[pair][:], in_=rms[pair][:])
 
-        def copy_x(j):
-            x_grouped[j] = stream.tile([P, P * PACK], BF16, name="x_grouped", align_bytes=64)
+        def transpose_x(pair):
+            x_t[pair] = psum.tile([P, PAIR, 2, P], F32, name="x_t")
+            for i in range(PAIR):
+                grp, row = divmod(pair * PAIR + i, GROUP)
+                words = x_sb[grp][:].bitcast(F32)
+                for u in range(2):
+                    first = row * (E // 2) + u
+                    nc.tensor.transpose(
+                        x_t[pair][:, i, u, :], words[:, first : (row + 1) * (E // 2) : 2], identity[:]
+                    )
+
+        def copy_x(pair):
+            x_grouped[pair] = stream.tile([P, PAIR * P * PACK], BF16, name="x_grouped", align_bytes=64)
             nc.scalar.copy(
-                out=x_grouped[j][:].bitcast(F32).rearrange("p (r u) -> p r u", u=2),
-                in_=x_t[j][:].rearrange("p u r -> p r u"),
+                out=x_grouped[pair][:].bitcast(F32).rearrange("p (i r u) -> p i r u", i=PAIR, u=2),
+                in_=x_t[pair][:].rearrange("p i u r -> p i r u"),
             )
 
-        def quantise_x(j):
-            x_codes[j] = stream.tile([P, P], U32, name="x_codes", align_bytes=64)
-            x_scales[j] = stream.tile([P, P], U8, name="x_scales", align_bytes=64)
+        def quantise_x(pair):
+            x_codes[pair] = stream.tile([P, PAIR * P], U32, name="x_codes", align_bytes=64)
+            x_scales[pair] = stream.tile([P, PAIR * P], U8, name="x_scales", align_bytes=64)
             nc.vector.quantize_mx(
-                out=x_codes[j][:].bitcast(FP8X4), scales=x_scales[j][:], in_=x_grouped[j][:]
+                out=x_codes[pair][:].bitcast(FP8X4), scales=x_scales[pair][:], in_=x_grouped[pair][:]
             )
 
-        def gate_matmul(j):
-            g_ps[j] = []
-            for n in range(F_BANKS):
-                cols = slice(n * BANK, (n + 1) * BANK)
-                bank = psum.tile([P, BANK], F32, name="g_ps")
-                nc.tensor.matmul_mx(
-                    out=bank[:],
-                    lhsT=x_codes[j][:].bitcast(FP8X4),
-                    lhsT_scale=x_scales[j][:],
-                    rhs=wg_codes[:, cols].bitcast(FP8X4),
-                    rhs_scale=wg_scales[:, cols],
-                    start=True,
-                    stop=True,
-                )
-                g_ps[j].append(bank)
+        def gate_matmul(j, n):
+            pair, i = divmod(j, PAIR)
+            tokens = slice(i * P, (i + 1) * P)
+            cols = slice(n * BANK, (n + 1) * BANK)
+            g_ps[j, n] = psum.tile([P, BANK], F32, name="g_ps", bufs=3)
+            nc.tensor.matmul_mx(
+                out=g_ps[j, n][:],
+                lhsT=x_codes[pair][:, tokens].bitcast(FP8X4),
+                lhsT_scale=x_scales[pair][:, tokens],
+                rhs=wg_codes[:, cols].bitcast(FP8X4),
+                rhs_scale=wg_scales[:, cols],
+                start=True,
+                stop=True,
+            )
 
-        def gate_multiply(j):
+        def weigh_o(j):
             grp, i = divmod(j, GROUP)
-            h_f32[j] = stream.tile([P, F], F32, name="h_f32")
-            for head in range(HEADS):
-                n, a = divmod(head, HEADS_PER_BANK)
-                rows = slice(a * HEAD_ROWS, (a + 1) * HEAD_ROWS)
-                o_head = o_sb[grp][:, i * F + head * DV : i * F + (head + 1) * DV]
-                h_bank = h_f32[j][:, n * BANK : (n + 1) * BANK]
+            o_gn[j] = stream.tile([P, BANK], F32, name="o_gn", bufs=1)
+            nc.gpsimd.tensor_tensor(
+                out=o_gn[j][:].rearrange("p (u m e) -> p u m e", u=2, e=2),
+                in0=o_sb[grp][:, i * F : i * F + BANK].rearrange("p (m u e) -> p u m e", u=2, e=2),
+                in1=gn_pairs[:].rearrange("p (u m e) -> p u m e", u=2, e=2),
+                op=mult,
+            )
+
+        def gate_pairs(j):
+            h_pairs[j] = stream.tile([P, BANK], BF16, name="h_pairs", align_bytes=64)
+            for a in range(HEADS_PER_PASS):
+                cols = slice(a * P, (a + 1) * P)
                 nc.vector.scalar_tensor_tensor(
-                    out=h_bank.rearrange("p (t m) -> p t m", t=PACK)[:, :, rows],
-                    in0=g_ps[j][n][:].rearrange("p (t m) -> p t m", t=PACK)[:, :, rows],
-                    scalar=inv_rms[grp][:, i * HEADS + head : i * HEADS + head + 1],
-                    in1=o_head.rearrange("p (m t) -> p t m", t=PACK),
+                    out=pairs(h_pairs[j][:])[:, :, cols],
+                    in0=pairs(g_ps[j, 0][:])[:, :, cols],
+                    scalar=inv_rms_col(j, a),
+                    in1=pairs(o_gn[j][:])[:, :, cols],
                     op0=mult,
                     op1=mult,
                 )
 
-        def transpose_h(j):
-            h_t[j] = []
-            for c in range(F_PASSES):
-                bank = psum.tile([P, PACK, P], F32, name="h_t")
-                for t in range(PACK):
-                    first = c * K_PASS + t * P
-                    nc.tensor.transpose(
-                        bank[:, t, :], h_f32[j][:, first : first + P], identity[:]
-                    )
-                h_t[j].append(bank)
-
-        def scale_h(j):
-            h_grouped[j] = stream.tile([P, F_PASSES, P, PACK], BF16, name="h_grouped", align_bytes=64)
-            for c in range(F_PASSES):
-                nc.vector.tensor_tensor(
-                    out=h_grouped[j][:, c, :, :],
-                    in0=h_t[j][c][:].rearrange("p t r -> p r t"),
-                    in1=gn_word[:].unsqueeze(1).to_broadcast([P, P, PACK]),
-                    op=mult,
+        def gate_singles(j):
+            h_singles[j] = stream.tile([P, BANK], F32, name="h_singles")
+            for a in range(HEADS_PER_PASS):
+                rows = slice(a * HEAD_ROWS, (a + 1) * HEAD_ROWS)
+                nc.vector.scalar_tensor_tensor(
+                    out=h_singles[j][:].rearrange("p (t m) -> p t m", t=PACK)[:, :, rows],
+                    in0=g_ps[j, 1][:].rearrange("p (t m) -> p t m", t=PACK)[:, :, rows],
+                    scalar=inv_rms_col(j, HEADS_PER_PASS + a),
+                    in1=o_head(j, HEADS_PER_PASS + a).rearrange("p (m t) -> p t m", t=PACK),
+                    op0=mult,
+                    op1=mult,
                 )
 
+        def transpose_pairs(j):
+            hp_t[j] = psum.tile([P, 2, P], F32, name="hp_t")
+            words = h_pairs[j][:].bitcast(F32)
+            for u in range(2):
+                nc.tensor.transpose(hp_t[j][:, u, :], words[:, u * P : (u + 1) * P], identity[:])
+
+        def transpose_singles(j):
+            hs_t[j] = psum.tile([P, PACK, P], F32, name="hs_t")
+            for t in range(PACK):
+                nc.tensor.transpose(hs_t[j][:, t, :], h_singles[j][:, t * P : (t + 1) * P], identity[:])
+
+        def copy_pairs(j):
+            h_grouped[j] = stream.tile([P, 2, P, PACK], BF16, name="h_grouped", align_bytes=64)
+            copy = nc.vector.tensor_copy if j % 2 == 0 else nc.scalar.copy
+            copy(
+                out=h_grouped[j][:, 0, :, :]
+                .rearrange("p r t -> p (r t)")
+                .bitcast(F32)
+                .rearrange("p (r u) -> p r u", u=2),
+                in_=hp_t[j][:].rearrange("p u r -> p r u"),
+            )
+
+        def scale_singles(j):
+            nc.vector.tensor_tensor(
+                out=h_grouped[j][:, 1, :, :],
+                in0=hs_t[j][:].rearrange("p t r -> p r t"),
+                in1=gn_word[:].unsqueeze(1).to_broadcast([P, P, PACK]),
+                op=mult,
+            )
+
         def quantise_h(j):
-            h_codes[j] = stream.tile([P, F_PASSES * P], U32, name="h_codes", align_bytes=64)
-            h_scales[j] = stream.tile([P, F_PASSES * P], U8, name="h_scales", align_bytes=64)
+            h_codes[j] = stream.tile([P, 2 * P], U32, name="h_codes", align_bytes=64)
+            h_scales[j] = stream.tile([P, 2 * P], U8, name="h_scales", align_bytes=64)
             nc.vector.quantize_mx(
                 out=h_codes[j][:].bitcast(FP8X4),
                 scales=h_scales[j][:],
@@ -240,8 +293,8 @@ def tile_multiscaleretention_pc_t_kernel(tc, o_ret, x, Wg, gn_weight, Wo, out):
             )
 
         def out_matmul(j):
-            out_ps[j] = psum.tile([P, E], F32, name="out_ps")
-            for c in range(F_PASSES):
+            out_ps[j] = psum.tile([P, E], F32, name="out_ps", tag="out_ps", bufs=2)
+            for c in range(2):
                 tokens = slice(c * P, (c + 1) * P)
                 nc.tensor.matmul_mx(
                     out=out_ps[j][:],
@@ -250,37 +303,104 @@ def tile_multiscaleretention_pc_t_kernel(tc, o_ret, x, Wg, gn_weight, Wo, out):
                     rhs=wo_codes[:, c, :].bitcast(FP8X4),
                     rhs_scale=wo_scales[:, c, :],
                     start=(c == 0),
-                    stop=(c == F_PASSES - 1),
+                    stop=(c == 1),
                 )
 
         def copy_out(j):
             grp, i = divmod(j, GROUP)
-            out_sb = stream.tile([P, E], F32, name="out_sb")
+            out_sb = stream.tile([P, E], F32, name="out_sb", bufs=4)
             nc.scalar.copy(out=out_sb[:], in_=out_ps[j][:])
             nc.sync.dma_start(out=out_dram[grp][:, i * E : (i + 1) * E], in_=out_sb[:])
 
-        def run(stage, j):
-            if 0 <= j < TILES:
-                stage(j)
+        def in_range(j):
+            return 0 <= j < TILES
 
-        def pipeline_step(step):
-            run(transpose_x, step + X_TRANSPOSE_LEAD)
-            run(transpose_h, step + H_TRANSPOSE_LEAD)
-            run(copy_x, step + X_COPY_LEAD)
-            run(copy_out, step + OUT_COPY_LEAD)
-            run(sum_squares, step + SQUARES_LEAD)
-            run(gate_multiply, step + GATE_MULTIPLY_LEAD)
-            run(gate_matmul, step + GATE_MATMUL_LEAD)
-            run(invert_rms, step + INVERT_RMS_LEAD)
-            run(quantise_x, step + X_QUANTISE_LEAD)
-            run(quantise_h, step + H_QUANTISE_LEAD)
-            run(out_matmul, step + OUT_MATMUL_LEAD)
-            run(scale_h, step + H_SCALE_LEAD)
+        def pipeline_step(s):
+            if s % GROUP == 1 and 0 <= s // GROUP + 3 < GROUPS and s > 0:
+                load_x(s // GROUP + 3, 0, GROUP)
+                load_o(s // GROUP + 3, 0, GROUP)
+            if in_range(s):
+                gate_pairs(s)
+            if in_range(s + 1):
+                gate_matmul(s + 1, 0)
+            if in_range(s - 2):
+                out_matmul(s - 2)
+            if in_range(s + 1):
+                gate_matmul(s + 1, 1)
+            if in_range(s - 1):
+                copy_pairs(s - 1)
+            if s % PAIR == 0 and in_range(s + 2):
+                copy_x((s + 2) // PAIR)
+            if in_range(s + 3):
+                sum_squares(s + 3, (0, 1))
+            if in_range(s - 2):
+                copy_out(s - 2)
+            if in_range(s + 3):
+                sum_squares(s + 3, (2, 3))
+                if s % PAIR == 0:
+                    root((s + 3) // PAIR)
+            if in_range(s - 1):
+                scale_singles(s - 1)
+            if in_range(s):
+                gate_singles(s)
+            if s % PAIR == 1 and in_range(s + 1):
+                invert((s + 1) // PAIR)
+            if in_range(s - 1):
+                quantise_h(s - 1)
+            if s % PAIR == 0 and in_range(s + 2):
+                quantise_x((s + 2) // PAIR)
+            if in_range(s + 1):
+                weigh_o(s + 1)
+            if in_range(s):
+                transpose_pairs(s)
+                transpose_singles(s)
+            if s % PAIR == 1 and in_range(s + 3):
+                transpose_x((s + 3) // PAIR)
 
         with tc.manual_schedule():
-            quantise_wg()
-            for step in range(FIRST_STEP, 1):
-                pipeline_step(step)
-            quantise_wo()
-            for step in range(1, LAST_STEP + 1):
-                pipeline_step(step)
+            nc.gpsimd.memset(gn_row[:], 0.0)
+            nc.gpsimd.memset(ones[:], 1.0)
+            nc.vector.memset(eps[:], EPS)
+            make_identity(nc, identity[:])
+            nc.scalar.activation(out=warm[:], in_=eps[:], func=func.Sqrt)
+
+            load_o(0, 0, 1)
+            load_wg(0)
+            load_x(0, 0, PAIR)
+            load_wg(1)
+            load_o(0, 1, PAIR)
+            load_small()
+            load_x(0, PAIR, GROUP)
+            load_o(0, PAIR, PAIR + 1)
+            load_wo(0)
+            load_wo(1)
+            load_o(0, PAIR + 1, GROUP)
+            for grp in range(1, 3):
+                load_x(grp, 0, GROUP)
+                load_o(grp, 0, GROUP)
+
+            sum_squares(0, (0, 1, 2, 3))
+            transpose_x(0)
+            copy_x(0)
+            group_wg_pairs()
+            group_wg_singles()
+            quantise_wg(0)
+            quantise_x(0)
+            gate_matmul(0, 0)
+            sum_squares(1, (0, 1, 2, 3))
+            root(0)
+            spread_gn()
+            weigh_o(0)
+            quantise_wg(1)
+            gate_matmul(0, 1)
+            invert(0)
+            transpose_x(1)
+            sum_squares(2, (0, 1, 2, 3))
+            pipeline_step(0)
+            group_wo(0)
+            group_wo(1)
+            pipeline_step(1)
+            quantise_wo(0)
+            quantise_wo(1)
+            for s in range(2, TILES + 2):
+                pipeline_step(s)

@@ -54,7 +54,7 @@ def tile_multiscaleretention_pc_t_kernel(tc, o_ret, x, Wg, gn_weight, Wo, out):
         gn_word = keep.tile([P, PACK], BF16)
         gn_row = keep.tile([P, DV], BF16)
         ones = keep.tile([P, P], BF16)
-        gn_pairs = keep.tile([P, BANK], BF16)
+        gn_pairs = keep.tile([P, DV], BF16)
         identity = keep.tile([P, P], F32)
         eps = keep.tile([P, 1], F32)
         warm = keep.tile([P, 1], F32)
@@ -134,11 +134,10 @@ def tile_multiscaleretention_pc_t_kernel(tc, o_ret, x, Wg, gn_weight, Wo, out):
         def spread_gn():
             spread = psum.tile([P, DV], F32, name="spread", tag="out_ps", bufs=2)
             nc.tensor.matmul(spread[:], lhsT=ones[:], rhs=gn_row[:], start=True, stop=True)
-            for a in range(HEADS_PER_PASS):
-                nc.scalar.copy(
-                    out=gn_pairs[:].rearrange("p (u a m e) -> p a u m e", u=2, a=2, e=2)[:, a],
-                    in_=spread[:].rearrange("p (m u e) -> p u m e", u=2, e=2),
-                )
+            nc.scalar.copy(
+                out=gn_pairs[:].rearrange("p (u m e) -> p u m e", u=2, e=2),
+                in_=spread[:].rearrange("p (m u e) -> p u m e", u=2, e=2),
+            )
 
         sums, rms, inv_rms = {}, {}, {}
         x_t, x_grouped, x_codes, x_scales = {}, {}, {}, {}
@@ -217,28 +216,27 @@ def tile_multiscaleretention_pc_t_kernel(tc, o_ret, x, Wg, gn_weight, Wo, out):
                 stop=True,
             )
 
-        def weigh_o(j):
-            grp, i = divmod(j, GROUP)
-            o_gn[j] = stream.tile([P, BANK], F32, name="o_gn", bufs=1)
+        def weigh_o(j, a):
+            o_gn[j, a] = stream.tile([P, DV], F32, name="o_gn%d" % a, bufs=1)
             nc.gpsimd.tensor_tensor(
-                out=o_gn[j][:].rearrange("p (u m e) -> p u m e", u=2, e=2),
-                in0=o_sb[grp][:, i * F : i * F + BANK].rearrange("p (m u e) -> p u m e", u=2, e=2),
+                out=o_gn[j, a][:].rearrange("p (u m e) -> p u m e", u=2, e=2),
+                in0=o_head(j, a).rearrange("p (m u e) -> p u m e", u=2, e=2),
                 in1=gn_pairs[:].rearrange("p (u m e) -> p u m e", u=2, e=2),
                 op=mult,
             )
 
-        def gate_pairs(j):
-            h_pairs[j] = stream.tile([P, BANK], BF16, name="h_pairs", align_bytes=64)
-            for a in range(HEADS_PER_PASS):
-                cols = slice(a * P, (a + 1) * P)
-                nc.vector.scalar_tensor_tensor(
-                    out=pairs(h_pairs[j][:])[:, :, cols],
-                    in0=pairs(g_ps[j, 0][:])[:, :, cols],
-                    scalar=inv_rms_col(j, a),
-                    in1=pairs(o_gn[j][:])[:, :, cols],
-                    op0=mult,
-                    op1=mult,
-                )
+        def gate_pairs(j, a):
+            if a == 0:
+                h_pairs[j] = stream.tile([P, BANK], BF16, name="h_pairs", align_bytes=64)
+            cols = slice(a * P, (a + 1) * P)
+            nc.vector.scalar_tensor_tensor(
+                out=pairs(h_pairs[j][:])[:, :, cols],
+                in0=pairs(g_ps[j, 0][:])[:, :, cols],
+                scalar=inv_rms_col(j, a),
+                in1=pairs(o_gn[j, a][:]),
+                op0=mult,
+                op1=mult,
+            )
 
         def gate_singles(j):
             h_singles[j] = stream.tile([P, BANK], F32, name="h_singles")
@@ -319,8 +317,11 @@ def tile_multiscaleretention_pc_t_kernel(tc, o_ret, x, Wg, gn_weight, Wo, out):
             if s % GROUP == 1 and 0 <= s // GROUP + 3 < GROUPS and s > 0:
                 load_x(s // GROUP + 3, 0, GROUP)
                 load_o(s // GROUP + 3, 0, GROUP)
-            if in_range(s):
-                gate_pairs(s)
+            for a in range(HEADS_PER_PASS):
+                if in_range(s):
+                    gate_pairs(s, a)
+                if in_range(s + 1):
+                    weigh_o(s + 1, a)
             if in_range(s + 1):
                 gate_matmul(s + 1, 0)
             if in_range(s - 2):
@@ -349,8 +350,6 @@ def tile_multiscaleretention_pc_t_kernel(tc, o_ret, x, Wg, gn_weight, Wo, out):
                 quantise_h(s - 1)
             if s % PAIR == 0 and in_range(s + 2):
                 quantise_x((s + 2) // PAIR)
-            if in_range(s + 1):
-                weigh_o(s + 1)
             if in_range(s):
                 transpose_pairs(s)
                 transpose_singles(s)
@@ -390,7 +389,8 @@ def tile_multiscaleretention_pc_t_kernel(tc, o_ret, x, Wg, gn_weight, Wo, out):
             sum_squares(1, (0, 1, 2, 3))
             root(0)
             spread_gn()
-            weigh_o(0)
+            weigh_o(0, 0)
+            weigh_o(0, 1)
             quantise_wg(1)
             gate_matmul(0, 1)
             invert(0)

@@ -54,7 +54,7 @@ def tile_multiscaleretention_pc_t_kernel(tc, o_ret, x, Wg, gn_weight, Wo, out):
         gn_word = keep.tile([P, PACK], BF16)
         gn_row = keep.tile([P, DV], BF16)
         ones = keep.tile([P, P], BF16)
-        gn_pairs = keep.tile([P, DV], BF16)
+        gn_all = keep.tile([P, DV], BF16)
         identity = keep.tile([P, P], F32)
         eps = keep.tile([P, 1], F32)
         warm = keep.tile([P, 1], F32)
@@ -93,17 +93,10 @@ def tile_multiscaleretention_pc_t_kernel(tc, o_ret, x, Wg, gn_weight, Wo, out):
                 out=wo_raw[c][:], in_=Wo.rearrange("(c p j) e -> c p j e", p=P, j=PACK)[c]
             )
 
-        def pairs(ap):
-            return ap.rearrange("p (u h) -> p u h", u=2)
-
         def group_wg_pairs():
-            for u in range(2):
-                nc.vector.tensor_copy(
-                    out=wg_grouped[:, u * DV : (u + 1) * DV, :].rearrange(
-                        "p (m e) j -> p m e j", e=2
-                    ),
-                    in_=wg_raw[0][:].rearrange("p j (m u e) -> p u m e j", u=2, e=2)[:, u],
-                )
+            nc.vector.tensor_copy(
+                out=wg_grouped[:, 0:BANK, :], in_=wg_raw[0][:].rearrange("p j f -> p f j")
+            )
 
         def group_wg_singles():
             nc.vector.tensor_copy(
@@ -134,10 +127,7 @@ def tile_multiscaleretention_pc_t_kernel(tc, o_ret, x, Wg, gn_weight, Wo, out):
         def spread_gn():
             spread = psum.tile([P, DV], F32, name="spread", tag="out_ps", bufs=2)
             nc.tensor.matmul(spread[:], lhsT=ones[:], rhs=gn_row[:], start=True, stop=True)
-            nc.scalar.copy(
-                out=gn_pairs[:].rearrange("p (u m e) -> p u m e", u=2, e=2),
-                in_=spread[:].rearrange("p (m u e) -> p u m e", u=2, e=2),
-            )
+            nc.scalar.copy(out=gn_all[:], in_=spread[:])
 
         sums, rms, inv_rms = {}, {}, {}
         x_t, x_grouped, x_codes, x_scales = {}, {}, {}, {}
@@ -218,22 +208,17 @@ def tile_multiscaleretention_pc_t_kernel(tc, o_ret, x, Wg, gn_weight, Wo, out):
 
         def weigh_o(j, a):
             o_gn[j, a] = stream.tile([P, DV], F32, name="o_gn%d" % a, bufs=1)
-            nc.gpsimd.tensor_tensor(
-                out=o_gn[j, a][:].rearrange("p (u m e) -> p u m e", u=2, e=2),
-                in0=o_head(j, a).rearrange("p (m u e) -> p u m e", u=2, e=2),
-                in1=gn_pairs[:].rearrange("p (u m e) -> p u m e", u=2, e=2),
-                op=mult,
-            )
+            nc.gpsimd.tensor_tensor(out=o_gn[j, a][:], in0=o_head(j, a), in1=gn_all[:], op=mult)
 
         def gate_pairs(j, a):
             if a == 0:
                 h_pairs[j] = stream.tile([P, BANK], BF16, name="h_pairs", align_bytes=64)
-            cols = slice(a * P, (a + 1) * P)
+            cols = slice(a * DV, (a + 1) * DV)
             nc.vector.scalar_tensor_tensor(
-                out=pairs(h_pairs[j][:])[:, :, cols],
-                in0=pairs(g_ps[j, 0][:])[:, :, cols],
+                out=h_pairs[j][:, cols],
+                in0=g_ps[j, 0][:, cols],
                 scalar=inv_rms_col(j, a),
-                in1=pairs(o_gn[j, a][:]),
+                in1=o_gn[j, a][:],
                 op0=mult,
                 op1=mult,
             )
@@ -255,7 +240,7 @@ def tile_multiscaleretention_pc_t_kernel(tc, o_ret, x, Wg, gn_weight, Wo, out):
             hp_t[j] = psum.tile([P, 2, P], F32, name="hp_t")
             words = h_pairs[j][:].bitcast(F32)
             for u in range(2):
-                nc.tensor.transpose(hp_t[j][:, u, :], words[:, u * P : (u + 1) * P], identity[:])
+                nc.tensor.transpose(hp_t[j][:, u, :], words[:, u::2], identity[:])
 
         def transpose_singles(j):
             hs_t[j] = psum.tile([P, PACK, P], F32, name="hs_t")

@@ -79,8 +79,10 @@ def tile_multiscaleretention_pc_t_kernel(tc, o_ret, x, Wg, gn_weight, Wo, out):
                 out=wg_raw[n][:], in_=Wg.rearrange("(p j) f -> p j f", j=PACK)[:, :, cols]
             )
 
-        def load_small():
+        def load_gn_row():
             nc.sync.dma_start(out=gn_row[0:1, :], in_=gn_weight.unsqueeze(0))
+
+        def load_gn_word():
             with nc.allow_non_contiguous_dma(reason="4 elements to a partition"):
                 for a in range(HEADS_PER_PASS):
                     nc.sync.dma_start(
@@ -212,6 +214,7 @@ def tile_multiscaleretention_pc_t_kernel(tc, o_ret, x, Wg, gn_weight, Wo, out):
 
         def gate_pairs(j, a):
             if a == 0:
+                h_grouped[j] = stream.tile([P, 2, P, PACK], BF16, name="h_grouped", align_bytes=64)
                 h_pairs[j] = stream.tile([P, BANK], BF16, name="h_pairs", align_bytes=64)
             cols = slice(a * DV, (a + 1) * DV)
             nc.vector.scalar_tensor_tensor(
@@ -248,7 +251,6 @@ def tile_multiscaleretention_pc_t_kernel(tc, o_ret, x, Wg, gn_weight, Wo, out):
                 nc.tensor.transpose(hs_t[j][:, t, :], h_singles[j][:, t * P : (t + 1) * P], identity[:])
 
         def copy_pairs(j):
-            h_grouped[j] = stream.tile([P, 2, P, PACK], BF16, name="h_grouped", align_bytes=64)
             copy = nc.vector.tensor_copy if j % 2 == 0 else nc.scalar.copy
             copy(
                 out=h_grouped[j][:, 0, :, :]
@@ -269,31 +271,41 @@ def tile_multiscaleretention_pc_t_kernel(tc, o_ret, x, Wg, gn_weight, Wo, out):
         def quantise_h(j):
             h_codes[j] = stream.tile([P, 2 * P], U32, name="h_codes", align_bytes=64)
             h_scales[j] = stream.tile([P, 2 * P], U8, name="h_scales", align_bytes=64)
-            nc.vector.quantize_mx(
-                out=h_codes[j][:].bitcast(FP8X4),
-                scales=h_scales[j][:],
-                in_=h_grouped[j][:].rearrange("p c r t -> p (c r t)"),
-            )
+            passes_at_once = 1 if j == TILES - 1 else 2
+            for c in range(0, 2, passes_at_once):
+                cols = slice(c * P, (c + passes_at_once) * P)
+                nc.vector.quantize_mx(
+                    out=h_codes[j][:, cols].bitcast(FP8X4),
+                    scales=h_scales[j][:, cols],
+                    in_=h_grouped[j][:, c : c + passes_at_once].rearrange("p c r t -> p (c r t)"),
+                )
 
         def out_matmul(j):
-            out_ps[j] = psum.tile([P, E], F32, name="out_ps", tag="out_ps", bufs=2)
-            for c in range(2):
-                tokens = slice(c * P, (c + 1) * P)
-                nc.tensor.matmul_mx(
-                    out=out_ps[j][:],
-                    lhsT=h_codes[j][:, tokens].bitcast(FP8X4),
-                    lhsT_scale=h_scales[j][:, tokens],
-                    rhs=wo_codes[:, c, :].bitcast(FP8X4),
-                    rhs_scale=wo_scales[:, c, :],
-                    start=(c == 0),
-                    stop=(c == 1),
-                )
+            width = E // 2 if j == TILES - 1 else E
+            for first in range(0, E, width):
+                cols = slice(first, first + width)
+                bank = psum.tile([P, width], F32, name="out_ps", tag="out_ps", bufs=2)
+                for c in range(2):
+                    tokens = slice(c * P, (c + 1) * P)
+                    nc.tensor.matmul_mx(
+                        out=bank[:],
+                        lhsT=h_codes[j][:, tokens].bitcast(FP8X4),
+                        lhsT_scale=h_scales[j][:, tokens],
+                        rhs=wo_codes[:, c, cols].bitcast(FP8X4),
+                        rhs_scale=wo_scales[:, c, cols],
+                        start=(c == 0),
+                        stop=(c == 1),
+                    )
+                out_ps[j, first] = bank
 
         def copy_out(j):
             grp, i = divmod(j, GROUP)
-            out_sb = stream.tile([P, E], F32, name="out_sb", bufs=4)
-            nc.scalar.copy(out=out_sb[:], in_=out_ps[j][:])
-            nc.sync.dma_start(out=out_dram[grp][:, i * E : (i + 1) * E], in_=out_sb[:])
+            width = E // 2 if j == TILES - 1 else E
+            for first, copy in ((0, nc.scalar.copy), (E // 2, nc.vector.tensor_copy))[: E // width]:
+                out_sb = stream.tile([P, width], F32, name="out_sb", bufs=4)
+                copy(out=out_sb[:], in_=out_ps[j, first][:])
+                cols = slice(i * E + first, i * E + first + width)
+                nc.sync.dma_start(out=out_dram[grp][:, cols], in_=out_sb[:])
 
         def in_range(j):
             return 0 <= j < TILES
@@ -302,6 +314,10 @@ def tile_multiscaleretention_pc_t_kernel(tc, o_ret, x, Wg, gn_weight, Wo, out):
             if s % GROUP == 1 and 0 <= s // GROUP + 3 < GROUPS and s > 0:
                 load_x(s // GROUP + 3, 0, GROUP)
                 load_o(s // GROUP + 3, 0, GROUP)
+            last = s == TILES - 1
+            if last:
+                gate_singles(s)
+                scale_singles(s - 1)
             for a in range(HEADS_PER_PASS):
                 if in_range(s):
                     gate_pairs(s, a)
@@ -325,9 +341,9 @@ def tile_multiscaleretention_pc_t_kernel(tc, o_ret, x, Wg, gn_weight, Wo, out):
                 sum_squares(s + 3, (2, 3))
                 if s % PAIR == 0:
                     root((s + 3) // PAIR)
-            if in_range(s - 1):
+            if in_range(s - 1) and not last:
                 scale_singles(s - 1)
-            if in_range(s):
+            if in_range(s) and not last:
                 gate_singles(s)
             if s % PAIR == 1 and in_range(s + 1):
                 invert((s + 1) // PAIR)
@@ -336,8 +352,10 @@ def tile_multiscaleretention_pc_t_kernel(tc, o_ret, x, Wg, gn_weight, Wo, out):
             if s % PAIR == 0 and in_range(s + 2):
                 quantise_x((s + 2) // PAIR)
             if in_range(s):
-                transpose_pairs(s)
-                transpose_singles(s)
+                for transpose in (
+                    (transpose_singles, transpose_pairs) if last else (transpose_pairs, transpose_singles)
+                ):
+                    transpose(s)
             if s % PAIR == 1 and in_range(s + 3):
                 transpose_x((s + 3) // PAIR)
 
@@ -348,12 +366,13 @@ def tile_multiscaleretention_pc_t_kernel(tc, o_ret, x, Wg, gn_weight, Wo, out):
             make_identity(nc, identity[:])
             nc.scalar.activation(out=warm[:], in_=eps[:], func=func.Sqrt)
 
-            load_o(0, 0, 1)
             load_wg(0)
+            load_o(0, 0, 1)
+            load_gn_row()
             load_x(0, 0, PAIR)
             load_wg(1)
             load_o(0, 1, PAIR)
-            load_small()
+            load_gn_word()
             load_x(0, PAIR, GROUP)
             load_o(0, PAIR, PAIR + 1)
             load_wo(0)
@@ -363,17 +382,18 @@ def tile_multiscaleretention_pc_t_kernel(tc, o_ret, x, Wg, gn_weight, Wo, out):
                 load_x(grp, 0, GROUP)
                 load_o(grp, 0, GROUP)
 
-            sum_squares(0, (0, 1, 2, 3))
+            group_wg_pairs()
+            sum_squares(0, (0, 1))
+            spread_gn()
+            sum_squares(0, (2, 3))
             transpose_x(0)
             copy_x(0)
-            group_wg_pairs()
-            group_wg_singles()
             quantise_wg(0)
+            group_wg_singles()
             quantise_x(0)
             gate_matmul(0, 0)
             sum_squares(1, (0, 1, 2, 3))
             root(0)
-            spread_gn()
             weigh_o(0, 0)
             weigh_o(0, 1)
             quantise_wg(1)

@@ -54,7 +54,8 @@ def tile_multiscaleretention_pc_t_kernel(tc, o_ret, x, Wg, gn_weight, Wo, out):
         gn_word = keep.tile([P, PACK], BF16)
         gn_row = keep.tile([P, DV], BF16)
         ones = keep.tile([P, P], BF16)
-        gn_all = keep.tile([P, DV], BF16)
+        gn_all = keep.tile([P, HEADS_PER_PASS * DV], BF16)
+        work = [keep.tile([P, BANK], F32, name="work%d" % n, align_bytes=64) for n in range(3)]
         identity = keep.tile([P, P], F32)
         eps = keep.tile([P, 1], F32)
         warm = keep.tile([P, 1], F32)
@@ -129,7 +130,10 @@ def tile_multiscaleretention_pc_t_kernel(tc, o_ret, x, Wg, gn_weight, Wo, out):
         def spread_gn():
             spread = psum.tile([P, DV], F32, name="spread", tag="out_ps", bufs=2)
             nc.tensor.matmul(spread[:], lhsT=ones[:], rhs=gn_row[:], start=True, stop=True)
-            nc.scalar.copy(out=gn_all[:], in_=spread[:])
+            nc.scalar.copy(
+                out=gn_all[:].rearrange("p (a d) -> p a d", a=HEADS_PER_PASS),
+                in_=spread[:].unsqueeze(1).to_broadcast([P, HEADS_PER_PASS, DV]),
+            )
 
         sums, rms, inv_rms = {}, {}, {}
         x_t, x_grouped, x_codes, x_scales = {}, {}, {}, {}
@@ -208,20 +212,25 @@ def tile_multiscaleretention_pc_t_kernel(tc, o_ret, x, Wg, gn_weight, Wo, out):
                 stop=True,
             )
 
-        def weigh_o(j, a):
-            o_gn[j, a] = stream.tile([P, DV], F32, name="o_gn%d" % a, bufs=1)
-            nc.gpsimd.tensor_tensor(out=o_gn[j, a][:], in0=o_head(j, a), in1=gn_all[:], op=mult)
+        def weigh_o(j):
+            grp, i = divmod(j, GROUP)
+            o_gn[j] = work[j % 3]
+            nc.gpsimd.tensor_tensor(
+                out=o_gn[j][:], in0=o_sb[grp][:, i * F : i * F + BANK], in1=gn_all[:], op=mult
+            )
 
         def gate_pairs(j, a):
             if a == 0:
-                h_grouped[j] = stream.tile([P, 2, P, PACK], BF16, name="h_grouped", align_bytes=64)
+                h_grouped[j] = (
+                    work[j % 3][:].bitcast(BF16).rearrange("p (c r t) -> p c r t", c=2, t=PACK)
+                )
                 h_pairs[j] = stream.tile([P, BANK], BF16, name="h_pairs", align_bytes=64)
             cols = slice(a * DV, (a + 1) * DV)
             nc.vector.scalar_tensor_tensor(
                 out=h_pairs[j][:, cols],
                 in0=g_ps[j, 0][:, cols],
                 scalar=inv_rms_col(j, a),
-                in1=o_gn[j, a][:],
+                in1=o_gn[j][:, cols],
                 op0=mult,
                 op1=mult,
             )
@@ -253,7 +262,7 @@ def tile_multiscaleretention_pc_t_kernel(tc, o_ret, x, Wg, gn_weight, Wo, out):
         def copy_pairs(j):
             copy = nc.vector.tensor_copy if j % 2 == 0 else nc.scalar.copy
             copy(
-                out=h_grouped[j][:, 0, :, :]
+                out=h_grouped[j][:, 0]
                 .rearrange("p r t -> p (r t)")
                 .bitcast(F32)
                 .rearrange("p (r u) -> p r u", u=2),
@@ -262,7 +271,7 @@ def tile_multiscaleretention_pc_t_kernel(tc, o_ret, x, Wg, gn_weight, Wo, out):
 
         def scale_singles(j):
             nc.vector.tensor_tensor(
-                out=h_grouped[j][:, 1, :, :],
+                out=h_grouped[j][:, 1],
                 in0=hs_t[j][:].rearrange("p t r -> p r t"),
                 in1=gn_word[:].unsqueeze(1).to_broadcast([P, P, PACK]),
                 op=mult,
@@ -321,8 +330,6 @@ def tile_multiscaleretention_pc_t_kernel(tc, o_ret, x, Wg, gn_weight, Wo, out):
             for a in range(HEADS_PER_PASS):
                 if in_range(s):
                     gate_pairs(s, a)
-                if in_range(s + 1):
-                    weigh_o(s + 1, a)
             if in_range(s + 1):
                 gate_matmul(s + 1, 0)
             if in_range(s - 2):
@@ -347,10 +354,12 @@ def tile_multiscaleretention_pc_t_kernel(tc, o_ret, x, Wg, gn_weight, Wo, out):
                 gate_singles(s)
             if s % PAIR == 1 and in_range(s + 1):
                 invert((s + 1) // PAIR)
-            if in_range(s - 1):
-                quantise_h(s - 1)
             if s % PAIR == 0 and in_range(s + 2):
                 quantise_x((s + 2) // PAIR)
+            if in_range(s - 1):
+                quantise_h(s - 1)
+            if in_range(s + 2):
+                weigh_o(s + 2)
             if in_range(s):
                 for transpose in (
                     (transpose_singles, transpose_pairs) if last else (transpose_pairs, transpose_singles)
@@ -394,8 +403,8 @@ def tile_multiscaleretention_pc_t_kernel(tc, o_ret, x, Wg, gn_weight, Wo, out):
             gate_matmul(0, 0)
             sum_squares(1, (0, 1, 2, 3))
             root(0)
-            weigh_o(0, 0)
-            weigh_o(0, 1)
+            weigh_o(0)
+            weigh_o(1)
             quantise_wg(1)
             gate_matmul(0, 1)
             invert(0)

@@ -338,16 +338,14 @@ def tile_multiscaleretention_pc_t_kernel(tc, o_ret, x, Wg, gn_weight, Wo, out):
                 gate_matmul(s + 1, 1)
             if in_range(s - 1):
                 copy_pairs(s - 1)
-            if s % PAIR == 0 and in_range(s + 2):
-                copy_x((s + 2) // PAIR)
+            if s % PAIR == 1 and in_range(s + 3):
+                copy_x((s + 3) // PAIR)
             if in_range(s + 3):
-                sum_squares(s + 3, (0, 1))
-            if in_range(s - 2):
-                copy_out(s - 2)
-            if in_range(s + 3):
-                sum_squares(s + 3, (2, 3))
+                sum_squares(s + 3, (0, 1, 2, 3))
                 if s % PAIR == 0:
                     root((s + 3) // PAIR)
+            if in_range(s - 2):
+                copy_out(s - 2)
             if in_range(s - 1) and not last:
                 scale_singles(s - 1)
             if in_range(s) and not last:
@@ -365,8 +363,8 @@ def tile_multiscaleretention_pc_t_kernel(tc, o_ret, x, Wg, gn_weight, Wo, out):
                     (transpose_singles, transpose_pairs) if last else (transpose_pairs, transpose_singles)
                 ):
                     transpose(s)
-            if s % PAIR == 1 and in_range(s + 3):
-                transpose_x((s + 3) // PAIR)
+            if s % PAIR == 0 and in_range(s + 4):
+                transpose_x((s + 4) // PAIR)
 
         with tc.manual_schedule():
             nc.gpsimd.memset(gn_row[:], 0.0)
@@ -385,11 +383,13 @@ def tile_multiscaleretention_pc_t_kernel(tc, o_ret, x, Wg, gn_weight, Wo, out):
             load_x(0, PAIR, GROUP)
             load_o(0, PAIR, PAIR + 1)
             load_wo(0)
+            load_x(1, 0, PAIR)
             load_wo(1)
             load_o(0, PAIR + 1, GROUP)
-            for grp in range(1, 3):
-                load_x(grp, 0, GROUP)
-                load_o(grp, 0, GROUP)
+            load_x(1, PAIR, GROUP)
+            load_o(1, 0, GROUP)
+            load_x(2, 0, GROUP)
+            load_o(2, 0, GROUP)
 
             group_wg_pairs()
             sum_squares(0, (0, 1))
@@ -409,6 +409,7 @@ def tile_multiscaleretention_pc_t_kernel(tc, o_ret, x, Wg, gn_weight, Wo, out):
             gate_matmul(0, 1)
             invert(0)
             transpose_x(1)
+            copy_x(1)
             sum_squares(2, (0, 1, 2, 3))
             pipeline_step(0)
             group_wo(0)

@@ -135,7 +135,7 @@ def tile_multiscaleretention_pc_t_kernel(tc, o_ret, x, Wg, gn_weight, Wo, out):
                 in_=spread[:].unsqueeze(1).to_broadcast([P, HEADS_PER_PASS, DV]),
             )
 
-        sums, rms, inv_rms = {}, {}, {}
+        sums, inv_rms = {}, {}
         x_t, x_grouped, x_codes, x_scales = {}, {}, {}, {}
         g_ps, o_gn, h_pairs, h_singles, hp_t, hs_t = {}, {}, {}, {}, {}, {}
         h_grouped, h_codes, h_scales, out_ps = {}, {}, {}, {}
@@ -163,14 +163,14 @@ def tile_multiscaleretention_pc_t_kernel(tc, o_ret, x, Wg, gn_weight, Wo, out):
                 )
 
         def root(pair):
-            rms[pair] = stream.tile([P, PAIR * HEADS], F32, name="rms")
-            nc.scalar.activation(
-                out=rms[pair][:], in_=sums[pair][:], func=func.Sqrt, scale=1.0 / DV, bias=eps[:]
-            )
-
-        def invert(pair):
             inv_rms[pair] = stream.tile([P, PAIR * HEADS], F32, name="inv_rms")
-            nc.vector.reciprocal(out=inv_rms[pair][:], in_=rms[pair][:])
+            nc.scalar.activation(
+                out=inv_rms[pair][:],
+                in_=sums[pair][:],
+                func=func.Abs_reciprocal_sqrt,
+                scale=1.0 / DV,
+                bias=eps[:],
+            )
 
         def transpose_x(pair):
             x_t[pair] = psum.tile([P, PAIR, 2, P], F32, name="x_t")
@@ -342,16 +342,14 @@ def tile_multiscaleretention_pc_t_kernel(tc, o_ret, x, Wg, gn_weight, Wo, out):
                 copy_x((s + 3) // PAIR)
             if in_range(s + 3):
                 sum_squares(s + 3, (0, 1, 2, 3))
-                if s % PAIR == 0:
-                    root((s + 3) // PAIR)
             if in_range(s - 2):
                 copy_out(s - 2)
+            if s % PAIR == 0 and in_range(s + 3):
+                root((s + 3) // PAIR)
             if in_range(s - 1) and not last:
                 scale_singles(s - 1)
             if in_range(s) and not last:
                 gate_singles(s)
-            if s % PAIR == 1 and in_range(s + 1):
-                invert((s + 1) // PAIR)
             if s % PAIR == 0 and in_range(s + 2):
                 quantise_x((s + 2) // PAIR)
             if in_range(s - 1):
@@ -371,7 +369,7 @@ def tile_multiscaleretention_pc_t_kernel(tc, o_ret, x, Wg, gn_weight, Wo, out):
             nc.gpsimd.memset(ones[:], 1.0)
             nc.vector.memset(eps[:], EPS)
             make_identity(nc, identity[:])
-            nc.scalar.activation(out=warm[:], in_=eps[:], func=func.Sqrt)
+            nc.scalar.activation(out=warm[:], in_=eps[:], func=func.Abs_reciprocal_sqrt)
 
             load_wg(0)
             load_o(0, 0, 1)
@@ -407,7 +405,6 @@ def tile_multiscaleretention_pc_t_kernel(tc, o_ret, x, Wg, gn_weight, Wo, out):
             weigh_o(1)
             quantise_wg(1)
             gate_matmul(0, 1)
-            invert(0)
             transpose_x(1)
             copy_x(1)
             sum_squares(2, (0, 1, 2, 3))

@@ -27,6 +27,7 @@ GROUPS = TILES // GROUP
 PAIR = 2
 HEAD_ROWS = DV // PACK
 HEADS_PER_PASS = K_PASS // DV
+VECTOR_EVERY = 4
 
 FLOPS = 2 * TOKENS * E * F + 2 * TOKENS * F * E
 
@@ -115,10 +116,20 @@ def tile_multiscaleretention_pc_t_kernel(tc, o_ret, x, Wg, gn_weight, Wo, out):
                 in_=wg_grouped[:, cols, :].rearrange("p f t -> p (f t)"),
             )
 
-        def group_wo(c):
+        def group_wo():
             nc.vector.tensor_copy(
-                out=wo_grouped[:, c, :, :], in_=wo_raw[c][:].rearrange("p j e -> p e j")
+                out=wo_grouped[:, 0, :, :], in_=wo_raw[0][:].rearrange("p j e -> p e j")
             )
+            for quarter in range(4):
+                cols = slice(quarter * P, (quarter + 1) * P)
+                nc.gpsimd.tensor_scalar(
+                    out=wo_grouped[:, 1, cols, :],
+                    in0=wo_raw[1][:, :, cols].rearrange("p j e -> p e j"),
+                    scalar1=1.0,
+                    scalar2=0.0,
+                    op0=mult,
+                    op1=mybir.AluOpType.add,
+                )
 
         def quantise_wo(c):
             nc.vector.quantize_mx(
@@ -260,7 +271,7 @@ def tile_multiscaleretention_pc_t_kernel(tc, o_ret, x, Wg, gn_weight, Wo, out):
                 nc.tensor.transpose(hs_t[j][:, t, :], h_singles[j][:, t * P : (t + 1) * P], identity[:])
 
         def copy_pairs(j):
-            copy = nc.vector.tensor_copy if j % 2 == 0 else nc.scalar.copy
+            copy = nc.vector.tensor_copy if j % VECTOR_EVERY == 0 else nc.scalar.copy
             copy(
                 out=h_grouped[j][:, 0]
                 .rearrange("p r t -> p (r t)")
@@ -323,46 +334,44 @@ def tile_multiscaleretention_pc_t_kernel(tc, o_ret, x, Wg, gn_weight, Wo, out):
             if s % GROUP == 1 and 0 <= s // GROUP + 3 < GROUPS and s > 0:
                 load_x(s // GROUP + 3, 0, GROUP)
                 load_o(s // GROUP + 3, 0, GROUP)
-            last = s == TILES - 1
-            if last:
+            if in_range(s):
                 gate_singles(s)
+            if in_range(s - 1):
+                if (s - 1) % VECTOR_EVERY == 0:
+                    copy_pairs(s - 1)
                 scale_singles(s - 1)
-            for a in range(HEADS_PER_PASS):
-                if in_range(s):
-                    gate_pairs(s, a)
+            if in_range(s):
+                gate_pairs(s, 0)
+                gate_pairs(s, 1)
             if in_range(s + 1):
-                gate_matmul(s + 1, 0)
+                gate_matmul(s + 1, 1)
             if in_range(s - 2):
                 out_matmul(s - 2)
             if in_range(s + 1):
-                gate_matmul(s + 1, 1)
-            if in_range(s - 1):
+                gate_matmul(s + 1, 0)
+            if in_range(s + 3):
+                sum_squares(s + 3, (0, 1))
+            if in_range(s - 1) and (s - 1) % VECTOR_EVERY != 0:
                 copy_pairs(s - 1)
             if s % PAIR == 1 and in_range(s + 3):
                 copy_x((s + 3) // PAIR)
             if in_range(s + 3):
-                sum_squares(s + 3, (0, 1, 2, 3))
+                sum_squares(s + 3, (2, 3))
             if in_range(s - 2):
                 copy_out(s - 2)
             if s % PAIR == 0 and in_range(s + 3):
                 root((s + 3) // PAIR)
-            if in_range(s - 1) and not last:
-                scale_singles(s - 1)
-            if in_range(s) and not last:
-                gate_singles(s)
             if s % PAIR == 0 and in_range(s + 2):
                 quantise_x((s + 2) // PAIR)
             if in_range(s - 1):
                 quantise_h(s - 1)
             if in_range(s + 2):
                 weigh_o(s + 2)
-            if in_range(s):
-                for transpose in (
-                    (transpose_singles, transpose_pairs) if last else (transpose_pairs, transpose_singles)
-                ):
-                    transpose(s)
             if s % PAIR == 0 and in_range(s + 4):
                 transpose_x((s + 4) // PAIR)
+            if in_range(s):
+                transpose_singles(s)
+                transpose_pairs(s)
 
         with tc.manual_schedule():
             nc.gpsimd.memset(gn_row[:], 0.0)
@@ -371,11 +380,11 @@ def tile_multiscaleretention_pc_t_kernel(tc, o_ret, x, Wg, gn_weight, Wo, out):
             make_identity(nc, identity[:])
             nc.scalar.activation(out=warm[:], in_=eps[:], func=func.Abs_reciprocal_sqrt)
 
-            load_wg(0)
+            load_wg(1)
             load_o(0, 0, 1)
             load_gn_row()
             load_x(0, 0, PAIR)
-            load_wg(1)
+            load_wg(0)
             load_o(0, 1, PAIR)
             load_gn_word()
             load_x(0, PAIR, GROUP)
@@ -389,28 +398,27 @@ def tile_multiscaleretention_pc_t_kernel(tc, o_ret, x, Wg, gn_weight, Wo, out):
             load_x(2, 0, GROUP)
             load_o(2, 0, GROUP)
 
-            group_wg_pairs()
+            group_wg_singles()
             sum_squares(0, (0, 1))
             spread_gn()
             sum_squares(0, (2, 3))
             transpose_x(0)
             copy_x(0)
-            quantise_wg(0)
-            group_wg_singles()
+            quantise_wg(1)
+            group_wg_pairs()
             quantise_x(0)
-            gate_matmul(0, 0)
+            gate_matmul(0, 1)
             sum_squares(1, (0, 1, 2, 3))
             root(0)
             weigh_o(0)
             weigh_o(1)
-            quantise_wg(1)
-            gate_matmul(0, 1)
+            quantise_wg(0)
             transpose_x(1)
             copy_x(1)
+            gate_matmul(0, 0)
             sum_squares(2, (0, 1, 2, 3))
             pipeline_step(0)
-            group_wo(0)
-            group_wo(1)
+            group_wo()
             pipeline_step(1)
             quantise_wo(0)
             quantise_wo(1)

@@ -27,7 +27,7 @@ GROUPS = TILES // GROUP
 PAIR = 2
 HEAD_ROWS = DV // PACK
 HEADS_PER_PASS = K_PASS // DV
-VECTOR_EVERY = 4
+VECTOR_EVERY = 8
 
 FLOPS = 2 * TOKENS * E * F + 2 * TOKENS * F * E
 
@@ -116,10 +116,12 @@ def tile_multiscaleretention_pc_t_kernel(tc, o_ret, x, Wg, gn_weight, Wo, out):
                 in_=wg_grouped[:, cols, :].rearrange("p f t -> p (f t)"),
             )
 
-        def group_wo():
+        def group_wo_0():
             nc.vector.tensor_copy(
                 out=wo_grouped[:, 0, :, :], in_=wo_raw[0][:].rearrange("p j e -> p e j")
             )
+
+        def group_wo_1():
             for quarter in range(4):
                 cols = slice(quarter * P, (quarter + 1) * P)
                 nc.gpsimd.tensor_scalar(
@@ -361,6 +363,8 @@ def tile_multiscaleretention_pc_t_kernel(tc, o_ret, x, Wg, gn_weight, Wo, out):
                 copy_out(s - 2)
             if s % PAIR == 0 and in_range(s + 3):
                 root((s + 3) // PAIR)
+            if s == 0:
+                group_wo_0()
             if s % PAIR == 0 and in_range(s + 2):
                 quantise_x((s + 2) // PAIR)
             if in_range(s - 1):
@@ -391,10 +395,11 @@ def tile_multiscaleretention_pc_t_kernel(tc, o_ret, x, Wg, gn_weight, Wo, out):
             load_o(0, PAIR, PAIR + 1)
             load_wo(0)
             load_x(1, 0, PAIR)
-            load_wo(1)
             load_o(0, PAIR + 1, GROUP)
+            load_wo(1)
+            load_o(1, 0, PAIR)
             load_x(1, PAIR, GROUP)
-            load_o(1, 0, GROUP)
+            load_o(1, PAIR, GROUP)
             load_x(2, 0, GROUP)
             load_o(2, 0, GROUP)
 
@@ -413,12 +418,13 @@ def tile_multiscaleretention_pc_t_kernel(tc, o_ret, x, Wg, gn_weight, Wo, out):
             weigh_o(0)
             weigh_o(1)
             quantise_wg(0)
-            transpose_x(1)
-            copy_x(1)
             gate_matmul(0, 0)
-            sum_squares(2, (0, 1, 2, 3))
+            transpose_x(1)
+            sum_squares(2, (0, 1, 2))
+            copy_x(1)
+            sum_squares(2, (3,))
             pipeline_step(0)
-            group_wo()
+            group_wo_1()
             pipeline_step(1)
             quantise_wo(0)
             quantise_wo(1)

@@ -27,7 +27,7 @@ GROUPS = TILES // GROUP
 PAIR = 2
 HEAD_ROWS = DV // PACK
 HEADS_PER_PASS = K_PASS // DV
-VECTOR_EVERY = 8
+VECTOR_EVERY = 4
 
 FLOPS = 2 * TOKENS * E * F + 2 * TOKENS * F * E
 
@@ -97,10 +97,17 @@ def tile_multiscaleretention_pc_t_kernel(tc, o_ret, x, Wg, gn_weight, Wo, out):
                 out=wo_raw[c][:], in_=Wo.rearrange("(c p j) e -> c p j e", p=P, j=PACK)[c]
             )
 
+        def pairs(ap):
+            return ap.rearrange("p (u h) -> p u h", u=2)
+
         def group_wg_pairs():
-            nc.vector.tensor_copy(
-                out=wg_grouped[:, 0:BANK, :], in_=wg_raw[0][:].rearrange("p j f -> p f j")
-            )
+            for u in range(2):
+                nc.vector.tensor_copy(
+                    out=wg_grouped[:, u * DV : (u + 1) * DV, :].rearrange(
+                        "p (m e) j -> p m e j", e=2
+                    ),
+                    in_=wg_raw[0][:].rearrange("p j (m u e) -> p u m e j", u=2, e=2)[:, u],
+                )
 
         def group_wg_singles():
             nc.vector.tensor_copy(
@@ -143,10 +150,11 @@ def tile_multiscaleretention_pc_t_kernel(tc, o_ret, x, Wg, gn_weight, Wo, out):
         def spread_gn():
             spread = psum.tile([P, DV], F32, name="spread", tag="out_ps", bufs=2)
             nc.tensor.matmul(spread[:], lhsT=ones[:], rhs=gn_row[:], start=True, stop=True)
-            nc.scalar.copy(
-                out=gn_all[:].rearrange("p (a d) -> p a d", a=HEADS_PER_PASS),
-                in_=spread[:].unsqueeze(1).to_broadcast([P, HEADS_PER_PASS, DV]),
-            )
+            for a in range(HEADS_PER_PASS):
+                nc.scalar.copy(
+                    out=gn_all[:].rearrange("p (u a m e) -> p a u m e", u=2, a=2, e=2)[:, a],
+                    in_=spread[:].rearrange("p (m u e) -> p u m e", u=2, e=2),
+                )
 
         sums, inv_rms = {}, {}
         x_t, x_grouped, x_codes, x_scales = {}, {}, {}, {}
@@ -229,7 +237,10 @@ def tile_multiscaleretention_pc_t_kernel(tc, o_ret, x, Wg, gn_weight, Wo, out):
             grp, i = divmod(j, GROUP)
             o_gn[j] = work[j % 3]
             nc.gpsimd.tensor_tensor(
-                out=o_gn[j][:], in0=o_sb[grp][:, i * F : i * F + BANK], in1=gn_all[:], op=mult
+                out=o_gn[j][:].rearrange("p (u m e) -> p u m e", u=2, e=2),
+                in0=o_sb[grp][:, i * F : i * F + BANK].rearrange("p (m u e) -> p u m e", u=2, e=2),
+                in1=gn_all[:].rearrange("p (u m e) -> p u m e", u=2, e=2),
+                op=mult,
             )
 
         def gate_pairs(j, a):
@@ -238,12 +249,12 @@ def tile_multiscaleretention_pc_t_kernel(tc, o_ret, x, Wg, gn_weight, Wo, out):
                     work[j % 3][:].bitcast(BF16).rearrange("p (c r t) -> p c r t", c=2, t=PACK)
                 )
                 h_pairs[j] = stream.tile([P, BANK], BF16, name="h_pairs", align_bytes=64)
-            cols = slice(a * DV, (a + 1) * DV)
+            cols = slice(a * P, (a + 1) * P)
             nc.vector.scalar_tensor_tensor(
-                out=h_pairs[j][:, cols],
-                in0=g_ps[j, 0][:, cols],
+                out=pairs(h_pairs[j][:])[:, :, cols],
+                in0=pairs(g_ps[j, 0][:])[:, :, cols],
                 scalar=inv_rms_col(j, a),
-                in1=o_gn[j][:, cols],
+                in1=pairs(o_gn[j][:])[:, :, cols],
                 op0=mult,
                 op1=mult,
             )
@@ -265,7 +276,7 @@ def tile_multiscaleretention_pc_t_kernel(tc, o_ret, x, Wg, gn_weight, Wo, out):
             hp_t[j] = psum.tile([P, 2, P], F32, name="hp_t")
             words = h_pairs[j][:].bitcast(F32)
             for u in range(2):
-                nc.tensor.transpose(hp_t[j][:, u, :], words[:, u::2], identity[:])
+                nc.tensor.transpose(hp_t[j][:, u, :], words[:, u * P : (u + 1) * P], identity[:])
 
         def transpose_singles(j):
             hs_t[j] = psum.tile([P, PACK, P], F32, name="hs_t")

from contextlib import ExitStack

import concourse.mybir as mybir
from concourse.masks import make_identity

F32 = mybir.dt.float32
BF16 = mybir.dt.bfloat16
U32 = mybir.dt.uint32
U8 = mybir.dt.uint8
FP8X4 = mybir.dt.float8_e4m3fn_x4

P = 128
PACK = 4
K_PASS = P * PACK
BANK = 512

TOKENS = 4 * 1024
E = 512
HEADS = 4
DV = 256
F = HEADS * DV
EPS = 1e-5

TILES = TOKENS // P
GROUP = 4
GROUPS = TILES // GROUP
PAIR = 2
HEAD_ROWS = DV // PACK
HEADS_PER_PASS = K_PASS // DV
VECTOR_EVERY = 4

FLOPS = 2 * TOKENS * E * F + 2 * TOKENS * F * E


def tile_multiscaleretention_pc_t_kernel(tc, o_ret, x, Wg, gn_weight, Wo, out):
    nc = tc.nc
    mult = mybir.AluOpType.mult
    func = mybir.ActivationFunctionType

    x_dram = x.flatten_outer_dims().rearrange("(n p i) e -> n p (i e)", p=P, i=GROUP)
    o_dram = o_ret.rearrange("b t h d -> (b t) (h d)").rearrange(
        "(n p i) f -> n p (i f)", p=P, i=GROUP
    )
    out_dram = out.flatten_outer_dims().rearrange("(n p i) e -> n p (i e)", p=P, i=GROUP)

    with ExitStack() as ctx:
        keep = ctx.enter_context(tc.tile_pool(name="keep", bufs=1))
        stream = ctx.enter_context(tc.tile_pool(name="stream", bufs=3))
        psum = ctx.enter_context(tc.psum_pool(name="psum", bufs=1))

        x_sb = [keep.tile([P, GROUP * E], BF16, name="x_sb%d" % grp) for grp in range(GROUPS)]
        o_sb = [keep.tile([P, GROUP * F], BF16, name="o_sb%d" % grp) for grp in range(GROUPS)]
        wg_raw = [keep.tile([P, PACK, BANK], BF16, name="wg_raw%d" % n) for n in range(2)]
        wo_raw = [keep.tile([P, PACK, E], BF16, name="wo_raw%d" % c) for c in range(2)]
        gn_word = keep.tile([P, PACK], BF16)
        gn_row = keep.tile([P, DV], BF16)
        ones = keep.tile([P, P], BF16)
        gn_all = keep.tile([P, HEADS_PER_PASS * DV], BF16)
        work = [keep.tile([P, BANK], F32, name="work%d" % n, align_bytes=64) for n in range(3)]
        identity = keep.tile([P, P], F32)
        eps = keep.tile([P, 1], F32)
        warm = keep.tile([P, 1], F32)
        wg_grouped = keep.tile([P, F, PACK], BF16, align_bytes=64)
        wg_codes = keep.tile([P, F], U32, align_bytes=64)
        wg_scales = keep.tile([P, F], U8, align_bytes=64)
        wo_grouped = keep.tile([P, 2, E, PACK], BF16, align_bytes=64)
        wo_codes = keep.tile([P, 2, E], U32, align_bytes=64)
        wo_scales = keep.tile([P, 2, E], U8, align_bytes=64)

        def load_x(grp, first, last):
            cols = slice(first * E, last * E)
            nc.sync.dma_start(out=x_sb[grp][:, cols], in_=x_dram[grp][:, cols])

        def load_o(grp, first, last):
            cols = slice(first * F, last * F)
            nc.sync.dma_start(out=o_sb[grp][:, cols], in_=o_dram[grp][:, cols])

        def load_wg(n):
            cols = slice(n * BANK, (n + 1) * BANK)
            nc.sync.dma_start(
                out=wg_raw[n][:], in_=Wg.rearrange("(p j) f -> p j f", j=PACK)[:, :, cols]
            )

        def load_gn_row():
            nc.sync.dma_start(out=gn_row[0:1, :], in_=gn_weight.unsqueeze(0))

        def load_gn_word():
            with nc.allow_non_contiguous_dma(reason="4 elements to a partition"):
                for a in range(HEADS_PER_PASS):
                    nc.sync.dma_start(
                        out=gn_word[a * HEAD_ROWS : (a + 1) * HEAD_ROWS, :],
                        in_=gn_weight.rearrange("(p t) -> p t", t=PACK),
                    )

        def load_wo(c):
            nc.sync.dma_start(
                out=wo_raw[c][:], in_=Wo.rearrange("(c p j) e -> c p j e", p=P, j=PACK)[c]
            )

        def pairs(ap):
            return ap.rearrange("p (u h) -> p u h", u=2)

        def group_wg_pairs():
            for u in range(2):
                nc.vector.tensor_copy(
                    out=wg_grouped[:, u * DV : (u + 1) * DV, :].rearrange(
                        "p (m e) j -> p m e j", e=2
                    ),
                    in_=wg_raw[0][:].rearrange("p j (m u e) -> p u m e j", u=2, e=2)[:, u],
                )

        def group_wg_singles():
            nc.vector.tensor_copy(
                out=wg_grouped[:, BANK:F, :].rearrange("p (t m) j -> p t m j", t=PACK),
                in_=wg_raw[1][:].rearrange("p j (m t) -> p t m j", t=PACK),
            )

        def quantise_wg(n):
            cols = slice(n * BANK, (n + 1) * BANK)
            nc.vector.quantize_mx(
                out=wg_codes[:, cols].bitcast(FP8X4),
                scales=wg_scales[:, cols],
                in_=wg_grouped[:, cols, :].rearrange("p f t -> p (f t)"),
            )

        def group_wo_0():
            nc.vector.tensor_copy(
                out=wo_grouped[:, 0, :, :], in_=wo_raw[0][:].rearrange("p j e -> p e j")
            )

        def group_wo_1():
            for quarter in range(4):
                cols = slice(quarter * P, (quarter + 1) * P)
                nc.gpsimd.tensor_scalar(
                    out=wo_grouped[:, 1, cols, :],
                    in0=wo_raw[1][:, :, cols].rearrange("p j e -> p e j"),
                    scalar1=1.0,
                    scalar2=0.0,
                    op0=mult,
                    op1=mybir.AluOpType.add,
                )

        def quantise_wo(c):
            nc.vector.quantize_mx(
                out=wo_codes[:, c, :].bitcast(FP8X4),
                scales=wo_scales[:, c, :],
                in_=wo_grouped[:, c, :, :].rearrange("p e t -> p (e t)"),
            )

        def spread_gn():
            spread = psum.tile([P, DV], F32, name="spread", tag="out_ps", bufs=2)
            nc.tensor.matmul(spread[:], lhsT=ones[:], rhs=gn_row[:], start=True, stop=True)
            for a in range(HEADS_PER_PASS):
                nc.scalar.copy(
                    out=gn_all[:].rearrange("p (u a m e) -> p a u m e", u=2, a=2, e=2)[:, a],
                    in_=spread[:].rearrange("p (m u e) -> p u m e", u=2, e=2),
                )

        sums, inv_rms = {}, {}
        x_t, x_grouped, x_codes, x_scales = {}, {}, {}, {}
        g_ps, o_gn, h_pairs, h_singles, hp_t, hs_t = {}, {}, {}, {}, {}, {}
        h_grouped, h_codes, h_scales, out_ps = {}, {}, {}, {}

        def o_head(j, head):
            grp, i = divmod(j, GROUP)
            first = i * F + head * DV
            return o_sb[grp][:, first : first + DV]

        def inv_rms_col(j, head):
            pair, i = divmod(j, PAIR)
            return inv_rms[pair][:, i * HEADS + head : i * HEADS + head + 1]

        def sum_squares(j, heads):
            pair, i = divmod(j, PAIR)
            if i == 0 and heads[0] == 0:
                sums[pair] = stream.tile([P, PAIR * HEADS], F32, name="sums")
            for head in heads:
                squares = stream.tile([P, DV], BF16, name="squares")
                nc.scalar.activation(
                    out=squares[:],
                    in_=o_head(j, head),
                    func=func.Square,
                    accum_out=sums[pair][:, i * HEADS + head : i * HEADS + head + 1],
                )

        def root(pair):
            inv_rms[pair] = stream.tile([P, PAIR * HEADS], F32, name="inv_rms")
            nc.scalar.activation(
                out=inv_rms[pair][:],
                in_=sums[pair][:],
                func=func.Abs_reciprocal_sqrt,
                scale=1.0 / DV,
                bias=eps[:],
            )

        def transpose_x(pair):
            x_t[pair] = psum.tile([P, PAIR, 2, P], F32, name="x_t")
            for i in range(PAIR):
                grp, row = divmod(pair * PAIR + i, GROUP)
                words = x_sb[grp][:].bitcast(F32)
                for u in range(2):
                    first = row * (E // 2) + u
                    nc.tensor.transpose(
                        x_t[pair][:, i, u, :], words[:, first : (row + 1) * (E // 2) : 2], identity[:]
                    )

        def copy_x(pair):
            x_grouped[pair] = stream.tile([P, PAIR * P * PACK], BF16, name="x_grouped", align_bytes=64)
            nc.scalar.copy(
                out=x_grouped[pair][:].bitcast(F32).rearrange("p (i r u) -> p i r u", i=PAIR, u=2),
                in_=x_t[pair][:].rearrange("p i u r -> p i r u"),
            )

        def quantise_x(pair):
            x_codes[pair] = stream.tile([P, PAIR * P], U32, name="x_codes", align_bytes=64)
            x_scales[pair] = stream.tile([P, PAIR * P], U8, name="x_scales", align_bytes=64)
            nc.vector.quantize_mx(
                out=x_codes[pair][:].bitcast(FP8X4), scales=x_scales[pair][:], in_=x_grouped[pair][:]
            )

        def gate_matmul(j, n):
            pair, i = divmod(j, PAIR)
            tokens = slice(i * P, (i + 1) * P)
            cols = slice(n * BANK, (n + 1) * BANK)
            g_ps[j, n] = psum.tile([P, BANK], F32, name="g_ps", bufs=3)
            nc.tensor.matmul_mx(
                out=g_ps[j, n][:],
                lhsT=x_codes[pair][:, tokens].bitcast(FP8X4),
                lhsT_scale=x_scales[pair][:, tokens],
                rhs=wg_codes[:, cols].bitcast(FP8X4),
                rhs_scale=wg_scales[:, cols],
                start=True,
                stop=True,
            )

        def weigh_o(j):
            grp, i = divmod(j, GROUP)
            o_gn[j] = work[j % 3]
            nc.gpsimd.tensor_tensor(
                out=o_gn[j][:].rearrange("p (u m e) -> p u m e", u=2, e=2),
                in0=o_sb[grp][:, i * F : i * F + BANK].rearrange("p (m u e) -> p u m e", u=2, e=2),
                in1=gn_all[:].rearrange("p (u m e) -> p u m e", u=2, e=2),
                op=mult,
            )

        def gate_pairs(j, a):
            if a == 0:
                h_grouped[j] = (
                    work[j % 3][:].bitcast(BF16).rearrange("p (c r t) -> p c r t", c=2, t=PACK)
                )
                h_pairs[j] = stream.tile([P, BANK], BF16, name="h_pairs", align_bytes=64)
            cols = slice(a * P, (a + 1) * P)
            nc.vector.scalar_tensor_tensor(
                out=pairs(h_pairs[j][:])[:, :, cols],
                in0=pairs(g_ps[j, 0][:])[:, :, cols],
                scalar=inv_rms_col(j, a),
                in1=pairs(o_gn[j][:])[:, :, cols],
                op0=mult,
                op1=mult,
            )

        def gate_singles(j):
            h_singles[j] = stream.tile([P, BANK], F32, name="h_singles")
            for a in range(HEADS_PER_PASS):
                rows = slice(a * HEAD_ROWS, (a + 1) * HEAD_ROWS)
                nc.vector.scalar_tensor_tensor(
                    out=h_singles[j][:].rearrange("p (t m) -> p t m", t=PACK)[:, :, rows],
                    in0=g_ps[j, 1][:].rearrange("p (t m) -> p t m", t=PACK)[:, :, rows],
                    scalar=inv_rms_col(j, HEADS_PER_PASS + a),
                    in1=o_head(j, HEADS_PER_PASS + a).rearrange("p (m t) -> p t m", t=PACK),
                    op0=mult,
                    op1=mult,
                )

        def transpose_pairs(j):
            hp_t[j] = psum.tile([P, 2, P], F32, name="hp_t")
            words = h_pairs[j][:].bitcast(F32)
            for u in range(2):
                nc.tensor.transpose(hp_t[j][:, u, :], words[:, u * P : (u + 1) * P], identity[:])

        def transpose_singles(j):
            hs_t[j] = psum.tile([P, PACK, P], F32, name="hs_t")
            for t in range(PACK):
                nc.tensor.transpose(hs_t[j][:, t, :], h_singles[j][:, t * P : (t + 1) * P], identity[:])

        def copy_pairs(j):
            copy = nc.vector.tensor_copy if j % VECTOR_EVERY == 0 else nc.scalar.copy
            copy(
                out=h_grouped[j][:, 0]
                .rearrange("p r t -> p (r t)")
                .bitcast(F32)
                .rearrange("p (r u) -> p r u", u=2),
                in_=hp_t[j][:].rearrange("p u r -> p r u"),
            )

        def scale_singles(j):
            nc.vector.tensor_tensor(
                out=h_grouped[j][:, 1],
                in0=hs_t[j][:].rearrange("p t r -> p r t"),
                in1=gn_word[:].unsqueeze(1).to_broadcast([P, P, PACK]),
                op=mult,
            )

        def quantise_h(j):
            h_codes[j] = stream.tile([P, 2 * P], U32, name="h_codes", align_bytes=64)
            h_scales[j] = stream.tile([P, 2 * P], U8, name="h_scales", align_bytes=64)
            passes_at_once = 1 if j == TILES - 1 else 2
            for c in range(0, 2, passes_at_once):
                cols = slice(c * P, (c + passes_at_once) * P)
                nc.vector.quantize_mx(
                    out=h_codes[j][:, cols].bitcast(FP8X4),
                    scales=h_scales[j][:, cols],
                    in_=h_grouped[j][:, c : c + passes_at_once].rearrange("p c r t -> p (c r t)"),
                )

        def out_matmul(j):
            width = E // 2 if j == TILES - 1 else E
            for first in range(0, E, width):
                cols = slice(first, first + width)
                bank = psum.tile([P, width], F32, name="out_ps", tag="out_ps", bufs=2)
                for c in range(2):
                    tokens = slice(c * P, (c + 1) * P)
                    nc.tensor.matmul_mx(
                        out=bank[:],
                        lhsT=h_codes[j][:, tokens].bitcast(FP8X4),
                        lhsT_scale=h_scales[j][:, tokens],
                        rhs=wo_codes[:, c, cols].bitcast(FP8X4),
                        rhs_scale=wo_scales[:, c, cols],
                        start=(c == 0),
                        stop=(c == 1),
                    )
                out_ps[j, first] = bank

        def copy_out(j):
            grp, i = divmod(j, GROUP)
            width = E // 2 if j == TILES - 1 else E
            for first, copy in ((0, nc.scalar.copy), (E // 2, nc.vector.tensor_copy))[: E // width]:
                out_sb = stream.tile([P, width], F32, name="out_sb", bufs=4)
                copy(out=out_sb[:], in_=out_ps[j, first][:])
                cols = slice(i * E + first, i * E + first + width)
                nc.sync.dma_start(out=out_dram[grp][:, cols], in_=out_sb[:])

        def in_range(j):
            return 0 <= j < TILES

        def pipeline_step(s):
            if s % GROUP == 1 and 0 <= s // GROUP + 3 < GROUPS and s > 0:
                load_x(s // GROUP + 3, 0, GROUP)
                load_o(s // GROUP + 3, 0, GROUP)
            if in_range(s):
                gate_singles(s)
            if in_range(s - 1):
                if (s - 1) % VECTOR_EVERY == 0:
                    copy_pairs(s - 1)
                scale_singles(s - 1)
            if in_range(s):
                gate_pairs(s, 0)
                gate_pairs(s, 1)
            if in_range(s + 1):
                gate_matmul(s + 1, 1)
            if in_range(s - 2):
                out_matmul(s - 2)
            if in_range(s + 1):
                gate_matmul(s + 1, 0)
            if in_range(s + 3):
                sum_squares(s + 3, (0, 1))
            if in_range(s - 1) and (s - 1) % VECTOR_EVERY != 0:
                copy_pairs(s - 1)
            if s % PAIR == 1 and in_range(s + 3):
                copy_x((s + 3) // PAIR)
            if in_range(s + 3):
                sum_squares(s + 3, (2, 3))
            if in_range(s - 2):
                copy_out(s - 2)
            if s % PAIR == 0 and in_range(s + 3):
                root((s + 3) // PAIR)
            if s == 0:
                group_wo_0()
            if s % PAIR == 0 and in_range(s + 2):
                quantise_x((s + 2) // PAIR)
            if in_range(s - 1):
                quantise_h(s - 1)
            if in_range(s + 2):
                weigh_o(s + 2)
            if s % PAIR == 0 and in_range(s + 4):
                transpose_x((s + 4) // PAIR)
            if in_range(s):
                transpose_singles(s)
                transpose_pairs(s)

        with tc.manual_schedule():
            nc.gpsimd.memset(gn_row[:], 0.0)
            nc.gpsimd.memset(ones[:], 1.0)
            nc.vector.memset(eps[:], EPS)
            make_identity(nc, identity[:])
            nc.scalar.activation(out=warm[:], in_=eps[:], func=func.Abs_reciprocal_sqrt)

            load_wg(1)
            load_o(0, 0, 1)
            load_gn_row()
            load_x(0, 0, PAIR)
            load_wg(0)
            load_o(0, 1, PAIR)
            load_gn_word()
            load_x(0, PAIR, GROUP)
            load_o(0, PAIR, PAIR + 1)
            load_wo(0)
            load_x(1, 0, PAIR)
            load_o(0, PAIR + 1, GROUP)
            load_wo(1)
            load_o(1, 0, PAIR)
            load_x(1, PAIR, GROUP)
            load_o(1, PAIR, GROUP)
            load_x(2, 0, GROUP)
            load_o(2, 0, GROUP)

            group_wg_singles()
            sum_squares(0, (0, 1))
            spread_gn()
            sum_squares(0, (2, 3))
            transpose_x(0)
            copy_x(0)
            quantise_wg(1)
            group_wg_pairs()
            quantise_x(0)
            gate_matmul(0, 1)
            sum_squares(1, (0, 1, 2, 3))
            root(0)
            weigh_o(0)
            weigh_o(1)
            quantise_wg(0)
            gate_matmul(0, 0)
            transpose_x(1)
            sum_squares(2, (0, 1, 2))
            copy_x(1)
            sum_squares(2, (3,))
            pipeline_step(0)
            group_wo_1()
            pipeline_step(1)
            quantise_wo(0)
            quantise_wo(1)
            for s in range(2, TILES + 2):
                pipeline_step(s)
